import numpy as np
import ml_dtypes


def mxq(x, axis, fmt="e4m3"):
    dtype, down = {"e4m3": (ml_dtypes.float8_e4m3fn, 7), "e5m2": (ml_dtypes.float8_e5m2, 14)}[fmt]
    v = np.moveaxis(np.asarray(x, np.float32).astype(ml_dtypes.bfloat16).astype(np.float64), axis, -1)
    blocks = v.reshape(v.shape[:-1] + (-1, 32))
    amax = np.abs(blocks).max(-1, keepdims=True)
    byte = np.maximum(np.where(amax > 0, np.frexp(amax)[1] - 1 + 127, 0) - down, 1)
    scale = np.exp2(byte - 127.0)
    codes = (blocks / scale).astype(np.float32).astype(dtype).astype(np.float64)
    return np.moveaxis((codes * scale).reshape(v.shape), -1, axis)


WIDE = False


def mx_kscale(k):
    if not WIDE:
        return np.ones(k)
    levels = np.array([10, -10, 5, -5, 0])
    a = np.random.permutation(np.resize(levels, k // 512 * 4)).reshape(k // 512, 4)
    idx = np.arange(k)
    return np.exp2(a[idx // 512, idx % 128 // 32])


BF16 = ml_dtypes.bfloat16


def bf(x):
    return np.asarray(x, np.float32).astype(BF16)


def f64(x):
    return np.asarray(x).astype(np.float64)


B, S_T, S_C, H, D = 32, 256, 256, 2, 128


def setup_inputs():
    s = mx_kscale(S_T + S_C)
    r = s.max() / s.min()
    n = np.random.standard_normal
    return {"target_q": bf(n((B, S_T, H, D)) * 2.0),
            "target_k": bf(n((B, S_T, H, D))),
            "target_v": bf(n((B, S_T, H, D)) * 2.0),
            "cond_k": bf(n((B, S_C, H, D))),
            "cond_v": bf(n((B, S_C, H, D)) * 2.0 * r),
            "b_param": bf(1.0 + 0.25 * n(1) - np.log(r))}


def reference(target_q, target_k, target_v, cond_k, cond_v, b_param):
    q = f64(target_q)
    Bq, St, Hh, Dd = q.shape
    Sc = cond_k.shape[1]
    scale = Dd ** -0.5
    k_ext = np.concatenate([f64(target_k), f64(cond_k)], axis=1)
    v_ext = np.concatenate([f64(target_v), f64(cond_v)], axis=1)
    logits = (q.transpose(0, 2, 1, 3) @ k_ext.transpose(0, 2, 3, 1)) * scale
    bias = np.concatenate([np.zeros(St), np.broadcast_to(f64(b_param), (Sc,))])
    logits = logits + bias[None, None, None, :]
    e = np.exp(logits - logits.max(-1, keepdims=True))
    num = mxq(e, 3, "e4m3") @ mxq(v_ext.transpose(0, 2, 1, 3), 2, "e4m3")
    out = num / e.sum(-1, keepdims=True)
    return out.transpose(0, 2, 1, 3).reshape(Bq, St, Hh * Dd)

@@ -1,0 +1,274 @@
+from contextlib import ExitStack
+
+import concourse.mybir as mybir
+from concourse.masks import make_identity
+
+BF16 = mybir.dt.bfloat16
+F32 = mybir.dt.float32
+U32 = mybir.dt.uint32
+U8 = mybir.dt.uint8
+FP8X4 = mybir.dt.float8_e4m3fn_x4
+ALU = mybir.AluOpType
+ACTF = mybir.ActivationFunctionType
+AX = mybir.AxisListType
+
+B, S, H, D = 32, 256, 2, 128
+P = 128
+NHEADS = B * H
+SCALE = D ** -0.5
+FLOPS = 2 * 2 * B * H * S * (2 * S) * D
+
+CHUNKS = [1, 1, 2, 4, 4, 4, 4, 4, 4, 4]
+LD_BUFS = 4
+PIN = True
+V_ON_POOL = True
+
+
+def tile_easycontrolnetwork_t_kernel(tc, target_q, target_k, target_v, cond_k, cond_v, b_param, out):
+    nc = tc.nc
+    assert sum(CHUNKS) == B
+    starts = [sum(CHUNKS[:c]) for c in range(len(CHUNKS))]
+    where = {}
+    for c, nb in enumerate(CHUNKS):
+        for bi in range(nb):
+            where[starts[c] + bi] = (c, bi)
+
+    with ExitStack() as ctx:
+        const = ctx.enter_context(tc.tile_pool(name="const", bufs=1))
+        ld = ctx.enter_context(tc.tile_pool(name="ld", bufs=LD_BUFS))
+        work = ctx.enter_context(tc.tile_pool(name="work", bufs=3))
+        small = ctx.enter_context(tc.tile_pool(name="small", bufs=4))
+        ps_s = ctx.enter_context(tc.psum_pool(name="ps_s", bufs=4))
+        ps_1 = ctx.enter_context(tc.psum_pool(name="ps_1", bufs=1))
+
+        loaded = {}
+
+        def load(c):
+            b0, nb = starts[c], CHUNKS[c]
+            q = ld.tile([P, nb, 512], BF16, tag="q")
+            kt = ld.tile([P, nb, 512], BF16, tag="kt")
+            kc = ld.tile([P, nb, 512], BF16, tag="kc")
+            v = ld.tile([P, 2 * nb, 512], BF16, tag="v")
+            nc.sync.dma_start(out=q[:], in_=target_q[b0:b0 + nb].rearrange("b (r j) h d -> r b (j h d)", j=2))
+            nc.sync.dma_start(out=kt[:], in_=target_k[b0:b0 + nb].rearrange("b (r j) h d -> r b (j h d)", j=2))
+            nc.sync.dma_start(out=kc[:], in_=cond_k[b0:b0 + nb].rearrange("b (r j) h d -> r b (j h d)", j=2))
+            nc.sync.dma_start(out=v[0:64], in_=target_v[b0:b0 + nb].rearrange("b (g r j) h d -> r (b g) (j h d)", g=2, j=2))
+            nc.sync.dma_start(out=v[64:128], in_=cond_v[b0:b0 + nb].rearrange("b (g r j) h d -> r (b g) (j h d)", g=2, j=2))
+            loaded[c] = (q, kt, kc, v)
+
+        b_bf = const.tile([P, 1], BF16)
+        nc.scalar.dma_start(out=b_bf[:], in_=b_param.partition_broadcast(P))
+        for c in range(LD_BUFS):
+            load(c)
+
+        ident = const.tile([P, P], BF16)
+        make_identity(nc, ident[:])
+        b32 = const.tile([P, 1], F32)
+        nc.vector.tensor_copy(out=b32[:], in_=b_bf[:])
+        bvec = const.tile([P, 2, 2], F32)
+        nc.vector.memset(bvec[:], 0.0)
+        nc.vector.tensor_copy(out=bvec[:, 1, :], in_=b_bf[:, 0:1].to_broadcast([P, 2]))
+
+        if PIN:
+            ctx.enter_context(tc.manual_schedule())
+
+        st = {}
+
+        def ok(n):
+            return 0 <= n < NHEADS
+
+        def pe_qk_transposes(n):
+            b, h = divmod(n, 2)
+            c, bi = where[b]
+            q, kt, kc, v = loaded[c]
+            qkt_ps = ps_1.tile([P, 6, P], BF16, tag="qkt_ps")
+            for j in range(2):
+                o = j * 256 + h * 128
+                nc.tensor.transpose(qkt_ps[:, j, :], q[:, bi, o:o + 128], ident[:])
+            for j in range(2):
+                o = j * 256 + h * 128
+                nc.tensor.transpose(qkt_ps[:, 2 + 2 * j, :], kt[:, bi, o:o + 128], ident[:])
+                nc.tensor.transpose(qkt_ps[:, 3 + 2 * j, :], kc[:, bi, o:o + 128], ident[:])
+            st[("qkt_ps", n)] = qkt_ps
+
+        def act_qk_copy(n):
+            qkt = work.tile([P, 6, P], BF16, tag="qkt")
+            nc.scalar.copy(out=qkt[:], in_=st[("qkt_ps", n)][:])
+            st[("qkt", n)] = qkt
+
+        def pe_scores(n, jq):
+            qkt = st[("qkt", n)]
+            s_ps = ps_s.tile([P, 2, 2, 2, 64], F32, tag="s")
+            for g in range(2):
+                nc.tensor.matmul(
+                    s_ps[:, g].rearrange("q j y p -> q (j y) p"),
+                    lhsT=qkt[:, jq, :],
+                    rhs=qkt[:, 2:6, 64 * g:64 * g + 64],
+                    start=True,
+                    stop=True,
+                )
+            st[("s", n, jq)] = s_ps
+
+        def dve_max(n, jq):
+            if jq == 0:
+                mx = small.tile([P, 2, 2], F32, tag="mx")
+                st[("mx", n)] = mx
+            nc.vector.tensor_reduce(
+                out=st[("mx", n)][:, :, jq],
+                in_=st[("s", n, jq)][:].rearrange("q g j y p -> q y (g j) p"),
+                axis=AX.XY,
+                op=ALU.max,
+            )
+
+        def dve_bias_a(n):
+            cb = small.tile([P, 2], F32, tag="cb")
+            nc.vector.tensor_scalar(out=cb[:], in0=st[("mx", n)][:, 1, :], scalar1=SCALE, scalar2=b32[:, 0:1],
+                                    op0=ALU.mult, op1=ALU.add)
+            st[("cb", n)] = cb
+
+        def dve_bias_b(n):
+            m = small.tile([P, 2], F32, tag="m")
+            nc.vector.scalar_tensor_tensor(out=m[:], in0=st[("mx", n)][:, 0, :], scalar=SCALE, in1=st[("cb", n)][:],
+                                           op0=ALU.mult, op1=ALU.max)
+            st[("m", n)] = m
+
+        def dve_bias_c(n):
+            bias = small.tile([P, 2, 2], F32, tag="bias")
+            nc.vector.tensor_tensor(out=bias[:], in0=bvec[:], in1=st[("m", n)][:].unsqueeze(1).to_broadcast([P, 2, 2]),
+                                    op=ALU.subtract)
+            st[("bias", n)] = bias
+
+        def act_exp(n):
+            e = work.tile([P, 2, 4, 2, 64], BF16, tag="e")
+            rs = small.tile([P, 2, 2], F32, tag="rs")
+            bias = st[("bias", n)]
+            for jq in range(2):
+                s_v = st[("s", n, jq)][:].rearrange("q g j y p -> q (g j) y p")
+                for y in range(2):
+                    nc.scalar.activation(out=e[:, jq, :, y, :], in_=s_v[:, :, y, :], func=ACTF.Exp,
+                                         bias=bias[:, y, jq:jq + 1], scale=SCALE, accum_out=rs[:, jq, y:y + 1])
+            st[("e", n)] = e
+            st[("rs", n)] = rs
+
+        def pe_e_transposes(n):
+            e = st[("e", n)]
+            for jq in range(2):
+                et_ps = ps_1.tile([P, 4, P], BF16, tag="et%d" % jq, name="et%d" % jq)
+                for t in range(4):
+                    nc.tensor.transpose(et_ps[:, t, :], e[:, jq, t].rearrange("q y p -> q (y p)"), ident[:])
+                st[("et", n, jq)] = et_ps
+
+        def copy_et(n, jq):
+            if jq == 0:
+                eg = work.tile([P, 2, P, 4], BF16, tag="eg", align_bytes=64)
+                st[("eg", n)] = eg
+                nc.scalar.copy(out=eg[:, 0], in_=st[("et", n, 0)][:].rearrange("p t q -> p q t"))
+            else:
+                nc.vector.tensor_copy(out=st[("eg", n)][:, 1], in_=st[("et", n, 1)][:].rearrange("p t q -> p q t"))
+
+        def dve_quant_e(n):
+            ec = work.tile([P, 2 * P], U32, tag="ec", align_bytes=64)
+            es = work.tile([P, 2 * P], U8, tag="es", align_bytes=64)
+            nc.vector.quantize_mx(out=ec[:].bitcast(FP8X4), scales=es[:],
+                                  in_=st[("eg", n)][:].rearrange("p a q t -> p (a q t)"))
+            st[("ec", n)] = (ec, es)
+
+        def regroup_v(b):
+            c, bi = where[b]
+            v = loaded[c][3]
+            vg = work.tile([P, 2 * P, 4], BF16, tag="vg", align_bytes=64)
+            src = v[:, 2 * bi:2 * bi + 2, :].rearrange("p g (j c) -> p c (g j)", j=2)
+            if V_ON_POOL:
+                nc.gpsimd.tensor_scalar(out=vg[:], in0=src, scalar1=1.0, scalar2=0.0, op0=ALU.mult, op1=ALU.add)
+            else:
+                nc.vector.tensor_copy(out=vg[:], in_=src)
+            st[("vg", b)] = vg
+
+        def dve_quant_v(b):
+            vc = work.tile([P, 2 * P], U32, tag="vc", align_bytes=64)
+            vs = work.tile([P, 2 * P], U8, tag="vs", align_bytes=64)
+            nc.vector.quantize_mx(out=vc[:].bitcast(FP8X4), scales=vs[:],
+                                  in_=st[("vg", b)][:].rearrange("p c t -> p (c t)"))
+            st[("vc", b)] = (vc, vs)
+
+        def pe_pv(n):
+            b, h = divmod(n, 2)
+            ec, es = st[("ec", n)]
+            vc, vs = st[("vc", b)]
+            o_ps = ps_1.tile([P, 2, P], F32, tag="o_ps")
+            for jq in range(2):
+                nc.tensor.matmul_mx(
+                    out=o_ps[:, jq, :],
+                    lhsT=ec[:, 128 * jq:128 * jq + 128].bitcast(FP8X4),
+                    lhsT_scale=es[:, 128 * jq:128 * jq + 128],
+                    rhs=vc[:, 128 * h:128 * h + 128].bitcast(FP8X4),
+                    rhs_scale=vs[:, 128 * h:128 * h + 128],
+                    start=True,
+                    stop=True,
+                )
+            st[("o", n)] = o_ps
+
+        def dve_rsum(n):
+            rsum = small.tile([P, 2], F32, tag="rsum")
+            nc.vector.tensor_reduce(out=rsum[:], in_=st[("rs", n)][:], axis=AX.X, op=ALU.add)
+            st[("rsum", n)] = rsum
+
+        def dve_rinv(n):
+            rinv = small.tile([P, 2], F32, tag="rinv")
+            nc.vector.reciprocal(out=rinv[:], in_=st[("rsum", n)][:])
+            st[("rinv", n)] = rinv
+
+        def dve_norm(n):
+            b, h = divmod(n, 2)
+            if h == 0:
+                osb = work.tile([P, 2, 2 * P], F32, tag="osb")
+                st[("osb", b)] = osb
+            nc.vector.tensor_tensor(out=st[("osb", b)][:, :, 128 * h:128 * h + 128], in0=st[("o", n)][:],
+                                    in1=st[("rinv", n)][:].unsqueeze(2).to_broadcast([P, 2, P]), op=ALU.mult)
+            if h == 1:
+                nc.sync.dma_start(out=out[b].rearrange("(r j) c -> r (j c)", j=2),
+                                  in_=st[("osb", b)][:].rearrange("p j c -> p (j c)"))
+
+        last_head = {}
+        for c, nb in enumerate(CHUNKS):
+            last_head[2 * (starts[c] + nb) - 1] = c
+
+        for i in range(-1, NHEADS + 4):
+            if ok(i - 2):
+                pe_e_transposes(i - 2)
+            if ok(i + 1):
+                pe_qk_transposes(i + 1)
+            if ok(i - 1):
+                act_exp(i - 1)
+            if ok(i - 2):
+                copy_et(i - 2, 0)
+                copy_et(i - 2, 1)
+            if ok(i + 1):
+                act_qk_copy(i + 1)
+            if i % 2 == 1 and 0 <= (i + 1) // 2 < B:
+                regroup_v((i + 1) // 2)
+            if ok(i):
+                pe_scores(i, 0)
+            if ok(i - 3):
+                pe_pv(i - 3)
+            if ok(i):
+                pe_scores(i, 1)
+                dve_max(i, 0)
+                dve_max(i, 1)
+                dve_bias_a(i)
+            if ok(i - 2):
+                dve_quant_e(i - 2)
+            if ok(i):
+                dve_bias_b(i)
+            if ok(i - 2):
+                dve_rsum(i - 2)
+            if ok(i):
+                dve_bias_c(i)
+            if ok(i - 3):
+                dve_norm(i - 3)
+            if ok(i - 2):
+                dve_rinv(i - 2)
+            if i % 2 == 1 and 0 <= (i - 1) // 2 < B:
+                dve_quant_v((i - 1) // 2)
+            if (i + 1) in last_head and last_head[i + 1] + LD_BUFS < len(CHUNKS):
+                load(last_head[i + 1] + LD_BUFS)

@@ -21,7 +21,6 @@ FLOPS = 2 * 2 * B * H * S * (2 * S) * D
 CHUNKS = [1, 1, 2, 4, 4, 4, 4, 4, 4, 4]
 LD_BUFS = 4
 PIN = True
-V_ON_POOL = True
 
 
 def tile_easycontrolnetwork_t_kernel(tc, target_q, target_k, target_v, cond_k, cond_v, b_param, out):
@@ -38,6 +37,9 @@ def tile_easycontrolnetwork_t_kernel(tc, target_q, target_k, target_v, cond_k, c
         ld = ctx.enter_context(tc.tile_pool(name="ld", bufs=LD_BUFS))
         work = ctx.enter_context(tc.tile_pool(name="work", bufs=3))
         small = ctx.enter_context(tc.tile_pool(name="small", bufs=4))
+        vgp = ctx.enter_context(tc.tile_pool(name="vgp", bufs=1))
+        vqp = ctx.enter_context(tc.tile_pool(name="vqp", bufs=8))
+        eqp = ctx.enter_context(tc.tile_pool(name="eqp", bufs=4))
         ps_s = ctx.enter_context(tc.psum_pool(name="ps_s", bufs=4))
         ps_1 = ctx.enter_context(tc.psum_pool(name="ps_1", bufs=1))
 
@@ -63,8 +65,8 @@ def tile_easycontrolnetwork_t_kernel(tc, target_q, target_k, target_v, cond_k, c
 
         ident = const.tile([P, P], BF16)
         make_identity(nc, ident[:])
-        b32 = const.tile([P, 1], F32)
-        nc.vector.tensor_copy(out=b32[:], in_=b_bf[:])
+        bs = const.tile([P, 1], F32)
+        nc.vector.tensor_scalar(out=bs[:], in0=b_bf[:], scalar1=1.0 / SCALE, scalar2=None, op0=ALU.mult)
         bvec = const.tile([P, 2, 2], F32)
         nc.vector.memset(bvec[:], 0.0)
         nc.vector.tensor_copy(out=bvec[:, 1, :], in_=b_bf[:, 0:1].to_broadcast([P, 2]))
@@ -121,34 +123,31 @@ def tile_easycontrolnetwork_t_kernel(tc, target_q, target_k, target_v, cond_k, c
             )
 
         def dve_bias_a(n):
-            cb = small.tile([P, 2], F32, tag="cb")
-            nc.vector.tensor_scalar(out=cb[:], in0=st[("mx", n)][:, 1, :], scalar1=SCALE, scalar2=b32[:, 0:1],
-                                    op0=ALU.mult, op1=ALU.add)
-            st[("cb", n)] = cb
+            mraw = small.tile([P, 2], F32, tag="mraw")
+            nc.vector.scalar_tensor_tensor(out=mraw[:], in0=st[("mx", n)][:, 1, :], scalar=bs[:, 0:1],
+                                           in1=st[("mx", n)][:, 0, :], op0=ALU.add, op1=ALU.max)
+            st[("mraw", n)] = mraw
 
         def dve_bias_b(n):
-            m = small.tile([P, 2], F32, tag="m")
-            nc.vector.scalar_tensor_tensor(out=m[:], in0=st[("mx", n)][:, 0, :], scalar=SCALE, in1=st[("cb", n)][:],
-                                           op0=ALU.mult, op1=ALU.max)
-            st[("m", n)] = m
-
-        def dve_bias_c(n):
             bias = small.tile([P, 2, 2], F32, tag="bias")
-            nc.vector.tensor_tensor(out=bias[:], in0=bvec[:], in1=st[("m", n)][:].unsqueeze(1).to_broadcast([P, 2, 2]),
-                                    op=ALU.subtract)
+            nc.vector.scalar_tensor_tensor(out=bias[:], in0=st[("mraw", n)][:].unsqueeze(1).to_broadcast([P, 2, 2]),
+                                           scalar=-SCALE, in1=bvec[:], op0=ALU.mult, op1=ALU.add)
             st[("bias", n)] = bias
 
         def act_exp(n):
+            b, h = divmod(n, 2)
             e = work.tile([P, 2, 4, 2, 64], BF16, tag="e")
-            rs = small.tile([P, 2, 2], F32, tag="rs")
+            if h == 0:
+                rs = small.tile([P, 2, 2, 2], F32, tag="rs")
+                st[("rs", b)] = rs
+            rs = st[("rs", b)]
             bias = st[("bias", n)]
             for jq in range(2):
                 s_v = st[("s", n, jq)][:].rearrange("q g j y p -> q (g j) y p")
                 for y in range(2):
                     nc.scalar.activation(out=e[:, jq, :, y, :], in_=s_v[:, :, y, :], func=ACTF.Exp,
-                                         bias=bias[:, y, jq:jq + 1], scale=SCALE, accum_out=rs[:, jq, y:y + 1])
+                                         bias=bias[:, y, jq:jq + 1], scale=SCALE, accum_out=rs[:, h, jq, y:y + 1])
             st[("e", n)] = e
-            st[("rs", n)] = rs
 
         def pe_e_transposes(n):
             e = st[("e", n)]
@@ -167,108 +166,113 @@ def tile_easycontrolnetwork_t_kernel(tc, target_q, target_k, target_v, cond_k, c
                 nc.vector.tensor_copy(out=st[("eg", n)][:, 1], in_=st[("et", n, 1)][:].rearrange("p t q -> p q t"))
 
         def dve_quant_e(n):
-            ec = work.tile([P, 2 * P], U32, tag="ec", align_bytes=64)
-            es = work.tile([P, 2 * P], U8, tag="es", align_bytes=64)
+            ec = eqp.tile([P, 2 * P], U32, tag="ec", align_bytes=64)
+            es = eqp.tile([P, 2 * P], U8, tag="es", align_bytes=64)
             nc.vector.quantize_mx(out=ec[:].bitcast(FP8X4), scales=es[:],
                                   in_=st[("eg", n)][:].rearrange("p a q t -> p (a q t)"))
             st[("ec", n)] = (ec, es)
 
-        def regroup_v(b):
+        def pool_regroup_v(n):
+            b, h = divmod(n, 2)
             c, bi = where[b]
             v = loaded[c][3]
-            vg = work.tile([P, 2 * P, 4], BF16, tag="vg", align_bytes=64)
-            src = v[:, 2 * bi:2 * bi + 2, :].rearrange("p g (j c) -> p c (g j)", j=2)
-            if V_ON_POOL:
-                nc.gpsimd.tensor_scalar(out=vg[:], in0=src, scalar1=1.0, scalar2=0.0, op0=ALU.mult, op1=ALU.add)
-            else:
-                nc.vector.tensor_copy(out=vg[:], in_=src)
-            st[("vg", b)] = vg
+            vg = vgp.tile([P, P, 4], BF16, tag="vg", align_bytes=64)
+            src = v[:, 2 * bi:2 * bi + 2, :].rearrange("p g (j h d) -> p g j h d", j=2, h=2)[:, :, :, h, :]
+            nc.gpsimd.tensor_scalar(out=vg[:], in0=src.rearrange("p g j d -> p d (g j)"), scalar1=1.0, scalar2=0.0,
+                                    op0=ALU.mult, op1=ALU.add)
+            st[("vg", n)] = vg
 
-        def dve_quant_v(b):
-            vc = work.tile([P, 2 * P], U32, tag="vc", align_bytes=64)
-            vs = work.tile([P, 2 * P], U8, tag="vs", align_bytes=64)
+        def dve_quant_v(n):
+            vc = vqp.tile([P, P], U32, tag="vc", align_bytes=64)
+            vs = vqp.tile([P, P], U8, tag="vs", align_bytes=64)
             nc.vector.quantize_mx(out=vc[:].bitcast(FP8X4), scales=vs[:],
-                                  in_=st[("vg", b)][:].rearrange("p c t -> p (c t)"))
-            st[("vc", b)] = (vc, vs)
+                                  in_=st[("vg", n)][:].rearrange("p c t -> p (c t)"))
+            st[("vc", n)] = (vc, vs)
 
         def pe_pv(n):
-            b, h = divmod(n, 2)
             ec, es = st[("ec", n)]
-            vc, vs = st[("vc", b)]
+            vc, vs = st[("vc", n)]
             o_ps = ps_1.tile([P, 2, P], F32, tag="o_ps")
             for jq in range(2):
                 nc.tensor.matmul_mx(
                     out=o_ps[:, jq, :],
                     lhsT=ec[:, 128 * jq:128 * jq + 128].bitcast(FP8X4),
                     lhsT_scale=es[:, 128 * jq:128 * jq + 128],
-                    rhs=vc[:, 128 * h:128 * h + 128].bitcast(FP8X4),
-                    rhs_scale=vs[:, 128 * h:128 * h + 128],
+                    rhs=vc[:].bitcast(FP8X4),
+                    rhs_scale=vs[:],
                     start=True,
                     stop=True,
                 )
             st[("o", n)] = o_ps
 
-        def dve_rsum(n):
-            rsum = small.tile([P, 2], F32, tag="rsum")
-            nc.vector.tensor_reduce(out=rsum[:], in_=st[("rs", n)][:], axis=AX.X, op=ALU.add)
-            st[("rsum", n)] = rsum
+        def dve_rsum(b):
+            rsum = small.tile([P, 2, 2], F32, tag="rsum")
+            nc.vector.tensor_reduce(out=rsum[:], in_=st[("rs", b)][:], axis=AX.X, op=ALU.add)
+            st[("rsum", b)] = rsum
 
-        def dve_rinv(n):
-            rinv = small.tile([P, 2], F32, tag="rinv")
-            nc.vector.reciprocal(out=rinv[:], in_=st[("rsum", n)][:])
-            st[("rinv", n)] = rinv
+        def dve_rinv(b):
+            rinv = small.tile([P, 2, 2], F32, tag="rinv")
+            nc.vector.reciprocal(out=rinv[:], in_=st[("rsum", b)][:])
+            st[("rinv", b)] = rinv
 
-        def dve_norm(n):
+        def norm(n):
             b, h = divmod(n, 2)
+            rinv = st[("rinv", b)]
+            o_ps = st[("o", n)]
             if h == 0:
                 osb = work.tile([P, 2, 2 * P], F32, tag="osb")
                 st[("osb", b)] = osb
-            nc.vector.tensor_tensor(out=st[("osb", b)][:, :, 128 * h:128 * h + 128], in0=st[("o", n)][:],
-                                    in1=st[("rinv", n)][:].unsqueeze(2).to_broadcast([P, 2, P]), op=ALU.mult)
-            if h == 1:
+                for jq in range(2):
+                    nc.scalar.activation(out=osb[:, jq, 0:128], in_=o_ps[:, jq, :], func=ACTF.Copy,
+                                         scale=rinv[:, 0, jq:jq + 1])
+            else:
+                osb = st[("osb", b)]
+                nc.vector.tensor_tensor(out=osb[:, :, 128:256], in0=o_ps[:],
+                                        in1=rinv[:, 1, :].unsqueeze(2).to_broadcast([P, 2, P]), op=ALU.mult)
                 nc.sync.dma_start(out=out[b].rearrange("(r j) c -> r (j c)", j=2),
-                                  in_=st[("osb", b)][:].rearrange("p j c -> p (j c)"))
+                                  in_=osb[:].rearrange("p j c -> p (j c)"))
 
         last_head = {}
         for c, nb in enumerate(CHUNKS):
             last_head[2 * (starts[c] + nb) - 1] = c
 
-        for i in range(-1, NHEADS + 4):
+        for i in range(-2, NHEADS + 7):
             if ok(i - 2):
-                pe_e_transposes(i - 2)
-            if ok(i + 1):
-                pe_qk_transposes(i + 1)
-            if ok(i - 1):
-                act_exp(i - 1)
-            if ok(i - 2):
-                copy_et(i - 2, 0)
-                copy_et(i - 2, 1)
-            if ok(i + 1):
-                act_qk_copy(i + 1)
-            if i % 2 == 1 and 0 <= (i + 1) // 2 < B:
-                regroup_v((i + 1) // 2)
+                act_exp(i - 2)
             if ok(i):
                 pe_scores(i, 0)
-            if ok(i - 3):
-                pe_pv(i - 3)
+            if ok(i - 6):
+                pe_pv(i - 6)
             if ok(i):
                 pe_scores(i, 1)
+            if ok(i - 3):
+                pe_e_transposes(i - 3)
+                copy_et(i - 3, 0)
+            if ok(i + 1):
+                act_qk_copy(i + 1)
+            if ok(i + 2):
+                pe_qk_transposes(i + 2)
+            if ok(i - 6) and (i - 6) % 2 == 0:
+                norm(i - 6)
+            if ok(i):
                 dve_max(i, 0)
                 dve_max(i, 1)
                 dve_bias_a(i)
-            if ok(i - 2):
-                dve_quant_e(i - 2)
+            if ok(i - 6) and (i - 6) % 2 == 1:
+                norm(i - 6)
             if ok(i):
                 dve_bias_b(i)
-            if ok(i - 2):
-                dve_rsum(i - 2)
-            if ok(i):
-                dve_bias_c(i)
             if ok(i - 3):
-                dve_norm(i - 3)
-            if ok(i - 2):
-                dve_rinv(i - 2)
-            if i % 2 == 1 and 0 <= (i - 1) // 2 < B:
-                dve_quant_v((i - 1) // 2)
+                copy_et(i - 3, 1)
+            if i % 2 == 0 and 0 <= (i - 4) // 2 < B:
+                dve_rsum((i - 4) // 2)
+            if ok(i - 4):
+                dve_quant_e(i - 4)
+            if i % 2 == 0 and 0 <= (i - 4) // 2 < B:
+                dve_rinv((i - 4) // 2)
+            if ok(i):
+                dve_quant_v(i)
+            if ok(i + 1):
+                pool_regroup_v(i + 1)
             if (i + 1) in last_head and last_head[i + 1] + LD_BUFS < len(CHUNKS):
                 load(last_head[i + 1] + LD_BUFS)

@@ -38,7 +38,7 @@ def tile_easycontrolnetwork_t_kernel(tc, target_q, target_k, target_v, cond_k, c
         work = ctx.enter_context(tc.tile_pool(name="work", bufs=3))
         small = ctx.enter_context(tc.tile_pool(name="small", bufs=4))
         vgp = ctx.enter_context(tc.tile_pool(name="vgp", bufs=1))
-        vqp = ctx.enter_context(tc.tile_pool(name="vqp", bufs=8))
+        vqp = ctx.enter_context(tc.tile_pool(name="vqp", bufs=10))
         eqp = ctx.enter_context(tc.tile_pool(name="eqp", bufs=4))
         ps_s = ctx.enter_context(tc.psum_pool(name="ps_s", bufs=4))
         ps_1 = ctx.enter_context(tc.psum_pool(name="ps_1", bufs=1))
@@ -236,38 +236,39 @@ def tile_easycontrolnetwork_t_kernel(tc, target_q, target_k, target_v, cond_k, c
         for c, nb in enumerate(CHUNKS):
             last_head[2 * (starts[c] + nb) - 1] = c
 
-        for i in range(-2, NHEADS + 7):
+        for i in range(-2, NHEADS + 8):
             if ok(i - 2):
                 act_exp(i - 2)
+            if ok(i - 4):
+                copy_et(i - 4, 0)
+            if ok(i + 1):
+                act_qk_copy(i + 1)
+            if ok(i - 4):
+                copy_et(i - 4, 1)
             if ok(i):
                 pe_scores(i, 0)
-            if ok(i - 6):
-                pe_pv(i - 6)
+            if ok(i - 7):
+                pe_pv(i - 7)
             if ok(i):
                 pe_scores(i, 1)
             if ok(i - 3):
                 pe_e_transposes(i - 3)
-                copy_et(i - 3, 0)
-            if ok(i + 1):
-                act_qk_copy(i + 1)
             if ok(i + 2):
                 pe_qk_transposes(i + 2)
-            if ok(i - 6) and (i - 6) % 2 == 0:
-                norm(i - 6)
+            if ok(i - 7) and (i - 7) % 2 == 0:
+                norm(i - 7)
             if ok(i):
                 dve_max(i, 0)
                 dve_max(i, 1)
                 dve_bias_a(i)
-            if ok(i - 6) and (i - 6) % 2 == 1:
-                norm(i - 6)
+            if ok(i - 7) and (i - 7) % 2 == 1:
+                norm(i - 7)
             if ok(i):
                 dve_bias_b(i)
-            if ok(i - 3):
-                copy_et(i - 3, 1)
             if i % 2 == 0 and 0 <= (i - 4) // 2 < B:
                 dve_rsum((i - 4) // 2)
-            if ok(i - 4):
-                dve_quant_e(i - 4)
+            if ok(i - 5):
+                dve_quant_e(i - 5)
             if i % 2 == 0 and 0 <= (i - 4) // 2 < B:
                 dve_rinv((i - 4) // 2)
             if ok(i):

@@ -95,7 +95,10 @@ def tile_easycontrolnetwork_t_kernel(tc, target_q, target_k, target_v, cond_k, c
 
         def act_qk_copy(n):
             qkt = work.tile([P, 6, P], BF16, tag="qkt")
-            nc.scalar.copy(out=qkt[:], in_=st[("qkt_ps", n)][:])
+            if n % 2 == 0:
+                nc.scalar.copy(out=qkt[:], in_=st[("qkt_ps", n)][:])
+            else:
+                nc.vector.tensor_copy(out=qkt[:], in_=st[("qkt_ps", n)][:])
             st[("qkt", n)] = qkt
 
         def pe_scores(n, jq):
@@ -217,18 +220,13 @@ def tile_easycontrolnetwork_t_kernel(tc, target_q, target_k, target_v, cond_k, c
 
         def norm(n):
             b, h = divmod(n, 2)
-            rinv = st[("rinv", b)]
-            o_ps = st[("o", n)]
             if h == 0:
                 osb = work.tile([P, 2, 2 * P], F32, tag="osb")
                 st[("osb", b)] = osb
-                for jq in range(2):
-                    nc.scalar.activation(out=osb[:, jq, 0:128], in_=o_ps[:, jq, :], func=ACTF.Copy,
-                                         scale=rinv[:, 0, jq:jq + 1])
-            else:
-                osb = st[("osb", b)]
-                nc.vector.tensor_tensor(out=osb[:, :, 128:256], in0=o_ps[:],
-                                        in1=rinv[:, 1, :].unsqueeze(2).to_broadcast([P, 2, P]), op=ALU.mult)
+            osb = st[("osb", b)]
+            nc.vector.tensor_tensor(out=osb[:, :, 128 * h:128 * h + 128], in0=st[("o", n)][:],
+                                    in1=st[("rinv", b)][:, h, :].unsqueeze(2).to_broadcast([P, 2, P]), op=ALU.mult)
+            if h == 1:
                 nc.sync.dma_start(out=out[b].rearrange("(r j) c -> r (j c)", j=2),
                                   in_=osb[:].rearrange("p j c -> p (j c)"))
 
@@ -241,10 +239,9 @@ def tile_easycontrolnetwork_t_kernel(tc, target_q, target_k, target_v, cond_k, c
                 act_exp(i - 2)
             if ok(i - 4):
                 copy_et(i - 4, 0)
+                copy_et(i - 4, 1)
             if ok(i + 1):
                 act_qk_copy(i + 1)
-            if ok(i - 4):
-                copy_et(i - 4, 1)
             if ok(i):
                 pe_scores(i, 0)
             if ok(i - 7):
@@ -255,13 +252,11 @@ def tile_easycontrolnetwork_t_kernel(tc, target_q, target_k, target_v, cond_k, c
                 pe_e_transposes(i - 3)
             if ok(i + 2):
                 pe_qk_transposes(i + 2)
-            if ok(i - 7) and (i - 7) % 2 == 0:
-                norm(i - 7)
             if ok(i):
                 dve_max(i, 0)
                 dve_max(i, 1)
                 dve_bias_a(i)
-            if ok(i - 7) and (i - 7) % 2 == 1:
+            if ok(i - 7):
                 norm(i - 7)
             if ok(i):
                 dve_bias_b(i)

@@ -37,7 +37,7 @@ def tile_easycontrolnetwork_t_kernel(tc, target_q, target_k, target_v, cond_k, c
         ld = ctx.enter_context(tc.tile_pool(name="ld", bufs=LD_BUFS))
         work = ctx.enter_context(tc.tile_pool(name="work", bufs=3))
         small = ctx.enter_context(tc.tile_pool(name="small", bufs=4))
-        vgp = ctx.enter_context(tc.tile_pool(name="vgp", bufs=1))
+        vgp = ctx.enter_context(tc.tile_pool(name="vgp", bufs=2))
         vqp = ctx.enter_context(tc.tile_pool(name="vqp", bufs=10))
         eqp = ctx.enter_context(tc.tile_pool(name="eqp", bufs=4))
         ps_s = ctx.enter_context(tc.psum_pool(name="ps_s", bufs=4))
@@ -95,10 +95,7 @@ def tile_easycontrolnetwork_t_kernel(tc, target_q, target_k, target_v, cond_k, c
 
         def act_qk_copy(n):
             qkt = work.tile([P, 6, P], BF16, tag="qkt")
-            if n % 2 == 0:
-                nc.scalar.copy(out=qkt[:], in_=st[("qkt_ps", n)][:])
-            else:
-                nc.vector.tensor_copy(out=qkt[:], in_=st[("qkt_ps", n)][:])
+            nc.scalar.copy(out=qkt[:], in_=st[("qkt_ps", n)][:])
             st[("qkt", n)] = qkt
 
         def pe_scores(n, jq):
@@ -220,13 +217,18 @@ def tile_easycontrolnetwork_t_kernel(tc, target_q, target_k, target_v, cond_k, c
 
         def norm(n):
             b, h = divmod(n, 2)
+            rinv = st[("rinv", b)]
+            o_ps = st[("o", n)]
             if h == 0:
                 osb = work.tile([P, 2, 2 * P], F32, tag="osb")
                 st[("osb", b)] = osb
-            osb = st[("osb", b)]
-            nc.vector.tensor_tensor(out=osb[:, :, 128 * h:128 * h + 128], in0=st[("o", n)][:],
-                                    in1=st[("rinv", b)][:, h, :].unsqueeze(2).to_broadcast([P, 2, P]), op=ALU.mult)
-            if h == 1:
+                for jq in range(2):
+                    nc.scalar.activation(out=osb[:, jq, 0:128], in_=o_ps[:, jq, :], func=ACTF.Copy,
+                                         scale=rinv[:, 0, jq:jq + 1])
+            else:
+                osb = st[("osb", b)]
+                nc.vector.tensor_tensor(out=osb[:, :, 128:256], in0=o_ps[:],
+                                        in1=rinv[:, 1, :].unsqueeze(2).to_broadcast([P, 2, P]), op=ALU.mult)
                 nc.sync.dma_start(out=out[b].rearrange("(r j) c -> r (j c)", j=2),
                                   in_=osb[:].rearrange("p j c -> p (j c)"))
 
@@ -239,9 +241,10 @@ def tile_easycontrolnetwork_t_kernel(tc, target_q, target_k, target_v, cond_k, c
                 act_exp(i - 2)
             if ok(i - 4):
                 copy_et(i - 4, 0)
-                copy_et(i - 4, 1)
             if ok(i + 1):
                 act_qk_copy(i + 1)
+            if ok(i - 4):
+                copy_et(i - 4, 1)
             if ok(i):
                 pe_scores(i, 0)
             if ok(i - 7):
@@ -252,11 +255,13 @@ def tile_easycontrolnetwork_t_kernel(tc, target_q, target_k, target_v, cond_k, c
                 pe_e_transposes(i - 3)
             if ok(i + 2):
                 pe_qk_transposes(i + 2)
+            if ok(i - 7) and (i - 7) % 2 == 0:
+                norm(i - 7)
             if ok(i):
                 dve_max(i, 0)
                 dve_max(i, 1)
                 dve_bias_a(i)
-            if ok(i - 7):
+            if ok(i - 7) and (i - 7) % 2 == 1:
                 norm(i - 7)
             if ok(i):
                 dve_bias_b(i)

@@ -95,7 +95,10 @@ def tile_easycontrolnetwork_t_kernel(tc, target_q, target_k, target_v, cond_k, c
 
         def act_qk_copy(n):
             qkt = work.tile([P, 6, P], BF16, tag="qkt")
-            nc.scalar.copy(out=qkt[:], in_=st[("qkt_ps", n)][:])
+            if n % 2 == 0:
+                nc.scalar.copy(out=qkt[:], in_=st[("qkt_ps", n)][:])
+            else:
+                nc.vector.tensor_copy(out=qkt[:], in_=st[("qkt_ps", n)][:])
             st[("qkt", n)] = qkt
 
         def pe_scores(n, jq):
@@ -217,18 +220,13 @@ def tile_easycontrolnetwork_t_kernel(tc, target_q, target_k, target_v, cond_k, c
 
         def norm(n):
             b, h = divmod(n, 2)
-            rinv = st[("rinv", b)]
-            o_ps = st[("o", n)]
             if h == 0:
                 osb = work.tile([P, 2, 2 * P], F32, tag="osb")
                 st[("osb", b)] = osb
-                for jq in range(2):
-                    nc.scalar.activation(out=osb[:, jq, 0:128], in_=o_ps[:, jq, :], func=ACTF.Copy,
-                                         scale=rinv[:, 0, jq:jq + 1])
-            else:
-                osb = st[("osb", b)]
-                nc.vector.tensor_tensor(out=osb[:, :, 128:256], in0=o_ps[:],
-                                        in1=rinv[:, 1, :].unsqueeze(2).to_broadcast([P, 2, P]), op=ALU.mult)
+            osb = st[("osb", b)]
+            nc.vector.tensor_tensor(out=osb[:, :, 128 * h:128 * h + 128], in0=st[("o", n)][:],
+                                    in1=st[("rinv", b)][:, h, :].unsqueeze(2).to_broadcast([P, 2, P]), op=ALU.mult)
+            if h == 1:
                 nc.sync.dma_start(out=out[b].rearrange("(r j) c -> r (j c)", j=2),
                                   in_=osb[:].rearrange("p j c -> p (j c)"))
 
@@ -241,10 +239,9 @@ def tile_easycontrolnetwork_t_kernel(tc, target_q, target_k, target_v, cond_k, c
                 act_exp(i - 2)
             if ok(i - 4):
                 copy_et(i - 4, 0)
+                copy_et(i - 4, 1)
             if ok(i + 1):
                 act_qk_copy(i + 1)
-            if ok(i - 4):
-                copy_et(i - 4, 1)
             if ok(i):
                 pe_scores(i, 0)
             if ok(i - 7):
@@ -255,24 +252,22 @@ def tile_easycontrolnetwork_t_kernel(tc, target_q, target_k, target_v, cond_k, c
                 pe_e_transposes(i - 3)
             if ok(i + 2):
                 pe_qk_transposes(i + 2)
-            if ok(i - 7) and (i - 7) % 2 == 0:
-                norm(i - 7)
             if ok(i):
                 dve_max(i, 0)
                 dve_max(i, 1)
-                dve_bias_a(i)
-            if ok(i - 7) and (i - 7) % 2 == 1:
+            if ok(i - 7):
                 norm(i - 7)
             if ok(i):
-                dve_bias_b(i)
+                dve_bias_a(i)
             if i % 2 == 0 and 0 <= (i - 4) // 2 < B:
                 dve_rsum((i - 4) // 2)
             if ok(i - 5):
                 dve_quant_e(i - 5)
+            if ok(i):
+                dve_bias_b(i)
+                dve_quant_v(i)
             if i % 2 == 0 and 0 <= (i - 4) // 2 < B:
                 dve_rinv((i - 4) // 2)
-            if ok(i):
-                dve_quant_v(i)
             if ok(i + 1):
                 pool_regroup_v(i + 1)
             if (i + 1) in last_head and last_head[i + 1] + LD_BUFS < len(CHUNKS):

@@ -169,11 +169,14 @@ def tile_easycontrolnetwork_t_kernel(tc, target_q, target_k, target_v, cond_k, c
                 nc.vector.tensor_copy(out=st[("eg", n)][:, 1], in_=st[("et", n, 1)][:].rearrange("p t q -> p q t"))
 
         def dve_quant_e(n):
-            ec = eqp.tile([P, 2 * P], U32, tag="ec", align_bytes=64)
-            es = eqp.tile([P, 2 * P], U8, tag="es", align_bytes=64)
-            nc.vector.quantize_mx(out=ec[:].bitcast(FP8X4), scales=es[:],
+            b, h = divmod(n, 2)
+            if h == 0:
+                ec = eqp.tile([P, 4 * P], U32, tag="ec", align_bytes=64)
+                es = eqp.tile([P, 4 * P], U8, tag="es", align_bytes=64)
+                st[("ec", b)] = (ec, es)
+            ec, es = st[("ec", b)]
+            nc.vector.quantize_mx(out=ec[:, 256 * h:256 * h + 256].bitcast(FP8X4), scales=es[:, 256 * h:256 * h + 256],
                                   in_=st[("eg", n)][:].rearrange("p a q t -> p (a q t)"))
-            st[("ec", n)] = (ec, es)
 
         def pool_regroup_v(n):
             b, h = divmod(n, 2)
@@ -192,21 +195,31 @@ def tile_easycontrolnetwork_t_kernel(tc, target_q, target_k, target_v, cond_k, c
                                   in_=st[("vg", n)][:].rearrange("p c t -> p (c t)"))
             st[("vc", n)] = (vc, vs)
 
+        def pe_warm(n):
+            o_ps = ps_1.tile([P, 4, P], F32, tag="o_ps")
+            st[("o", n)] = o_ps
+            if n >= 1:
+                ec, es = st[("ec", (n - 1) // 2)]
+                vc, vs = st[("vc", n)]
+                nc.tensor.matmul_mx(out=o_ps[:].rearrange("q a d -> q (a d)"), lhsT=vc[:].bitcast(FP8X4), lhsT_scale=vs[:],
+                                    rhs=ec[:].bitcast(FP8X4), rhs_scale=es[:], start=True, stop=True)
+
         def pe_pv(n):
-            ec, es = st[("ec", n)]
+            b, h = divmod(n, 2)
+            ec, es = st[("ec", b)]
             vc, vs = st[("vc", n)]
-            o_ps = ps_1.tile([P, 2, P], F32, tag="o_ps")
+            o_ps = st[("o", n)]
             for jq in range(2):
+                c0 = 256 * h + 128 * jq
                 nc.tensor.matmul_mx(
                     out=o_ps[:, jq, :],
-                    lhsT=ec[:, 128 * jq:128 * jq + 128].bitcast(FP8X4),
-                    lhsT_scale=es[:, 128 * jq:128 * jq + 128],
+                    lhsT=ec[:, c0:c0 + 128].bitcast(FP8X4),
+                    lhsT_scale=es[:, c0:c0 + 128],
                     rhs=vc[:].bitcast(FP8X4),
                     rhs_scale=vs[:],
                     start=True,
                     stop=True,
                 )
-            st[("o", n)] = o_ps
 
         def dve_rsum(b):
             rsum = small.tile([P, 2, 2], F32, tag="rsum")
@@ -224,7 +237,7 @@ def tile_easycontrolnetwork_t_kernel(tc, target_q, target_k, target_v, cond_k, c
                 osb = work.tile([P, 2, 2 * P], F32, tag="osb")
                 st[("osb", b)] = osb
             osb = st[("osb", b)]
-            nc.vector.tensor_tensor(out=osb[:, :, 128 * h:128 * h + 128], in0=st[("o", n)][:],
+            nc.vector.tensor_tensor(out=osb[:, :, 128 * h:128 * h + 128], in0=st[("o", n)][:, 0:2, :],
                                     in1=st[("rinv", b)][:, h, :].unsqueeze(2).to_broadcast([P, 2, P]), op=ALU.mult)
             if h == 1:
                 nc.sync.dma_start(out=out[b].rearrange("(r j) c -> r (j c)", j=2),
@@ -257,6 +270,8 @@ def tile_easycontrolnetwork_t_kernel(tc, target_q, target_k, target_v, cond_k, c
                 dve_max(i, 1)
             if ok(i - 7):
                 norm(i - 7)
+            if ok(i - 6):
+                pe_warm(i - 6)
             if ok(i):
                 dve_bias_a(i)
             if i % 2 == 0 and 0 <= (i - 4) // 2 < B:

@@ -42,6 +42,7 @@ def tile_easycontrolnetwork_t_kernel(tc, target_q, target_k, target_v, cond_k, c
         eqp = ctx.enter_context(tc.tile_pool(name="eqp", bufs=4))
         ps_s = ctx.enter_context(tc.psum_pool(name="ps_s", bufs=4))
         ps_1 = ctx.enter_context(tc.psum_pool(name="ps_1", bufs=1))
+        ps_2 = ctx.enter_context(tc.psum_pool(name="ps_2", bufs=2))
 
         loaded = {}
 
@@ -67,9 +68,10 @@ def tile_easycontrolnetwork_t_kernel(tc, target_q, target_k, target_v, cond_k, c
         make_identity(nc, ident[:])
         bs = const.tile([P, 1], F32)
         nc.vector.tensor_scalar(out=bs[:], in0=b_bf[:], scalar1=1.0 / SCALE, scalar2=None, op0=ALU.mult)
-        bvec = const.tile([P, 2, 2], F32)
-        nc.vector.memset(bvec[:], 0.0)
-        nc.vector.tensor_copy(out=bvec[:, 1, :], in_=b_bf[:, 0:1].to_broadcast([P, 2]))
+        ident32 = const.tile([P, P], F32)
+        make_identity(nc, ident32[:])
+        bmat = const.tile([P, P], F32)
+        nc.vector.tensor_copy(out=bmat[:], in_=bs[:, 0:1].to_broadcast([P, P]))
 
         if PIN:
             ctx.enter_context(tc.manual_schedule())
@@ -89,94 +91,76 @@ def tile_easycontrolnetwork_t_kernel(tc, target_q, target_k, target_v, cond_k, c
                 nc.tensor.transpose(qkt_ps[:, j, :], q[:, bi, o:o + 128], ident[:])
             for j in range(2):
                 o = j * 256 + h * 128
-                nc.tensor.transpose(qkt_ps[:, 2 + 2 * j, :], kt[:, bi, o:o + 128], ident[:])
-                nc.tensor.transpose(qkt_ps[:, 3 + 2 * j, :], kc[:, bi, o:o + 128], ident[:])
+                nc.tensor.transpose(qkt_ps[:, 2 + j, :], kt[:, bi, o:o + 128], ident[:])
+                nc.tensor.transpose(qkt_ps[:, 4 + j, :], kc[:, bi, o:o + 128], ident[:])
             st[("qkt_ps", n)] = qkt_ps
 
         def act_qk_copy(n):
             qkt = work.tile([P, 6, P], BF16, tag="qkt")
-            if n % 2 == 0:
-                nc.scalar.copy(out=qkt[:], in_=st[("qkt_ps", n)][:])
-            else:
-                nc.vector.tensor_copy(out=qkt[:], in_=st[("qkt_ps", n)][:])
+            nc.vector.tensor_copy(out=qkt[:], in_=st[("qkt_ps", n)][:])
             st[("qkt", n)] = qkt
 
         def pe_scores(n, jq):
             qkt = st[("qkt", n)]
             s_ps = ps_s.tile([P, 2, 2, 2, 64], F32, tag="s")
             for g in range(2):
-                nc.tensor.matmul(
-                    s_ps[:, g].rearrange("q j y p -> q (j y) p"),
-                    lhsT=qkt[:, jq, :],
-                    rhs=qkt[:, 2:6, 64 * g:64 * g + 64],
-                    start=True,
-                    stop=True,
-                )
+                nc.tensor.matmul(s_ps[:, g, :, 1, :], lhsT=qkt[:, jq, :], rhs=qkt[:, 4:6, 64 * g:64 * g + 64],
+                                 start=True, stop=False)
+                nc.tensor.matmul(s_ps[:, g, :, 1, :], lhsT=bmat[:], rhs=ident32[:].rearrange("p (a c) -> p a c", a=2),
+                                 is_transpose=True, start=False, stop=True)
+                nc.tensor.matmul(s_ps[:, g, :, 0, :], lhsT=qkt[:, jq, :], rhs=qkt[:, 2:4, 64 * g:64 * g + 64],
+                                 start=True, stop=True)
             st[("s", n, jq)] = s_ps
 
         def dve_max(n, jq):
             if jq == 0:
-                mx = small.tile([P, 2, 2], F32, tag="mx")
+                mx = small.tile([P, 2], F32, tag="mx")
                 st[("mx", n)] = mx
             nc.vector.tensor_reduce(
-                out=st[("mx", n)][:, :, jq],
-                in_=st[("s", n, jq)][:].rearrange("q g j y p -> q y (g j) p"),
-                axis=AX.XY,
+                out=st[("mx", n)][:, jq:jq + 1],
+                in_=st[("s", n, jq)][:].rearrange("q g j y p -> q (g j y p)"),
+                axis=AX.X,
                 op=ALU.max,
             )
 
-        def dve_bias_a(n):
-            mraw = small.tile([P, 2], F32, tag="mraw")
-            nc.vector.scalar_tensor_tensor(out=mraw[:], in0=st[("mx", n)][:, 1, :], scalar=bs[:, 0:1],
-                                           in1=st[("mx", n)][:, 0, :], op0=ALU.add, op1=ALU.max)
-            st[("mraw", n)] = mraw
-
-        def dve_bias_b(n):
-            bias = small.tile([P, 2, 2], F32, tag="bias")
-            nc.vector.scalar_tensor_tensor(out=bias[:], in0=st[("mraw", n)][:].unsqueeze(1).to_broadcast([P, 2, 2]),
-                                           scalar=-SCALE, in1=bvec[:], op0=ALU.mult, op1=ALU.add)
-            st[("bias", n)] = bias
+        def dve_bias(n):
+            negm = small.tile([P, 2], F32, tag="negm")
+            nc.vector.tensor_scalar(out=negm[:], in0=st[("mx", n)][:], scalar1=-SCALE, scalar2=None, op0=ALU.mult)
+            st[("negm", n)] = negm
 
         def act_exp(n):
             b, h = divmod(n, 2)
-            e = work.tile([P, 2, 4, 2, 64], BF16, tag="e")
+            e = work.tile([P, 2, 4, P], BF16, tag="e")
             if h == 0:
-                rs = small.tile([P, 2, 2, 2], F32, tag="rs")
+                rs = small.tile([P, 2, 2], F32, tag="rs")
                 st[("rs", b)] = rs
             rs = st[("rs", b)]
-            bias = st[("bias", n)]
+            negm = st[("negm", n)]
             for jq in range(2):
-                s_v = st[("s", n, jq)][:].rearrange("q g j y p -> q (g j) y p")
-                for y in range(2):
-                    nc.scalar.activation(out=e[:, jq, :, y, :], in_=s_v[:, :, y, :], func=ACTF.Exp,
-                                         bias=bias[:, y, jq:jq + 1], scale=SCALE, accum_out=rs[:, h, jq, y:y + 1])
+                nc.scalar.activation(out=e[:, jq].rearrange("q t c -> q (t c)"),
+                                     in_=st[("s", n, jq)][:].rearrange("q g j y p -> q (g j y p)"), func=ACTF.Exp,
+                                     bias=negm[:, jq:jq + 1], scale=SCALE, accum_out=rs[:, h, jq:jq + 1])
             st[("e", n)] = e
 
         def pe_e_transposes(n):
             e = st[("e", n)]
+            et_ps = ps_2.tile([P, 2, 4, P], BF16, tag="et")
             for jq in range(2):
-                et_ps = ps_1.tile([P, 4, P], BF16, tag="et%d" % jq, name="et%d" % jq)
                 for t in range(4):
-                    nc.tensor.transpose(et_ps[:, t, :], e[:, jq, t].rearrange("q y p -> q (y p)"), ident[:])
-                st[("et", n, jq)] = et_ps
+                    nc.tensor.transpose(et_ps[:, jq, t, :], e[:, jq, t, :], ident[:])
+            st[("et", n)] = et_ps
 
-        def copy_et(n, jq):
-            if jq == 0:
-                eg = work.tile([P, 2, P, 4], BF16, tag="eg", align_bytes=64)
-                st[("eg", n)] = eg
-                nc.scalar.copy(out=eg[:, 0], in_=st[("et", n, 0)][:].rearrange("p t q -> p q t"))
-            else:
-                nc.vector.tensor_copy(out=st[("eg", n)][:, 1], in_=st[("et", n, 1)][:].rearrange("p t q -> p q t"))
+        def copy_et(n):
+            eg = work.tile([P, 2, P, 4], BF16, tag="eg", align_bytes=64)
+            st[("eg", n)] = eg
+            nc.scalar.copy(out=eg[:], in_=st[("et", n)][:].rearrange("p a t q -> p a q t"))
 
         def dve_quant_e(n):
-            b, h = divmod(n, 2)
-            if h == 0:
-                ec = eqp.tile([P, 4 * P], U32, tag="ec", align_bytes=64)
-                es = eqp.tile([P, 4 * P], U8, tag="es", align_bytes=64)
-                st[("ec", b)] = (ec, es)
-            ec, es = st[("ec", b)]
-            nc.vector.quantize_mx(out=ec[:, 256 * h:256 * h + 256].bitcast(FP8X4), scales=es[:, 256 * h:256 * h + 256],
+            ec = eqp.tile([P, 2 * P], U32, tag="ec", align_bytes=64)
+            es = eqp.tile([P, 2 * P], U8, tag="es", align_bytes=64)
+            nc.vector.quantize_mx(out=ec[:].bitcast(FP8X4), scales=es[:],
                                   in_=st[("eg", n)][:].rearrange("p a q t -> p (a q t)"))
+            st[("ec", n)] = (ec, es)
 
         def pool_regroup_v(n):
             b, h = divmod(n, 2)
@@ -195,40 +179,25 @@ def tile_easycontrolnetwork_t_kernel(tc, target_q, target_k, target_v, cond_k, c
                                   in_=st[("vg", n)][:].rearrange("p c t -> p (c t)"))
             st[("vc", n)] = (vc, vs)
 
-        def pe_warm(n):
-            o_ps = ps_1.tile([P, 4, P], F32, tag="o_ps")
-            st[("o", n)] = o_ps
-            if n >= 1:
-                ec, es = st[("ec", (n - 1) // 2)]
-                vc, vs = st[("vc", n)]
-                nc.tensor.matmul_mx(out=o_ps[:].rearrange("q a d -> q (a d)"), lhsT=vc[:].bitcast(FP8X4), lhsT_scale=vs[:],
-                                    rhs=ec[:].bitcast(FP8X4), rhs_scale=es[:], start=True, stop=True)
-
         def pe_pv(n):
-            b, h = divmod(n, 2)
-            ec, es = st[("ec", b)]
+            ec, es = st[("ec", n)]
             vc, vs = st[("vc", n)]
-            o_ps = st[("o", n)]
+            o_ps = ps_1.tile([P, 2, P], F32, tag="o_ps")
             for jq in range(2):
-                c0 = 256 * h + 128 * jq
                 nc.tensor.matmul_mx(
                     out=o_ps[:, jq, :],
-                    lhsT=ec[:, c0:c0 + 128].bitcast(FP8X4),
-                    lhsT_scale=es[:, c0:c0 + 128],
+                    lhsT=ec[:, 128 * jq:128 * jq + 128].bitcast(FP8X4),
+                    lhsT_scale=es[:, 128 * jq:128 * jq + 128],
                     rhs=vc[:].bitcast(FP8X4),
                     rhs_scale=vs[:],
                     start=True,
                     stop=True,
                 )
-
-        def dve_rsum(b):
-            rsum = small.tile([P, 2, 2], F32, tag="rsum")
-            nc.vector.tensor_reduce(out=rsum[:], in_=st[("rs", b)][:], axis=AX.X, op=ALU.add)
-            st[("rsum", b)] = rsum
+            st[("o", n)] = o_ps
 
         def dve_rinv(b):
             rinv = small.tile([P, 2, 2], F32, tag="rinv")
-            nc.vector.reciprocal(out=rinv[:], in_=st[("rsum", b)][:])
+            nc.vector.reciprocal(out=rinv[:], in_=st[("rs", b)][:])
             st[("rinv", b)] = rinv
 
         def norm(n):
@@ -237,7 +206,7 @@ def tile_easycontrolnetwork_t_kernel(tc, target_q, target_k, target_v, cond_k, c
                 osb = work.tile([P, 2, 2 * P], F32, tag="osb")
                 st[("osb", b)] = osb
             osb = st[("osb", b)]
-            nc.vector.tensor_tensor(out=osb[:, :, 128 * h:128 * h + 128], in0=st[("o", n)][:, 0:2, :],
+            nc.vector.tensor_tensor(out=osb[:, :, 128 * h:128 * h + 128], in0=st[("o", n)][:],
                                     in1=st[("rinv", b)][:, h, :].unsqueeze(2).to_broadcast([P, 2, P]), op=ALU.mult)
             if h == 1:
                 nc.sync.dma_start(out=out[b].rearrange("(r j) c -> r (j c)", j=2),
@@ -251,8 +220,7 @@ def tile_easycontrolnetwork_t_kernel(tc, target_q, target_k, target_v, cond_k, c
             if ok(i - 2):
                 act_exp(i - 2)
             if ok(i - 4):
-                copy_et(i - 4, 0)
-                copy_et(i - 4, 1)
+                copy_et(i - 4)
             if ok(i + 1):
                 act_qk_copy(i + 1)
             if ok(i):
@@ -270,19 +238,14 @@ def tile_easycontrolnetwork_t_kernel(tc, target_q, target_k, target_v, cond_k, c
                 dve_max(i, 1)
             if ok(i - 7):
                 norm(i - 7)
-            if ok(i - 6):
-                pe_warm(i - 6)
             if ok(i):
-                dve_bias_a(i)
-            if i % 2 == 0 and 0 <= (i - 4) // 2 < B:
-                dve_rsum((i - 4) // 2)
+                dve_bias(i)
             if ok(i - 5):
                 dve_quant_e(i - 5)
-            if ok(i):
-                dve_bias_b(i)
-                dve_quant_v(i)
             if i % 2 == 0 and 0 <= (i - 4) // 2 < B:
                 dve_rinv((i - 4) // 2)
+            if ok(i):
+                dve_quant_v(i)
             if ok(i + 1):
                 pool_regroup_v(i + 1)
             if (i + 1) in last_head and last_head[i + 1] + LD_BUFS < len(CHUNKS):

@@ -49,14 +49,14 @@ def tile_easycontrolnetwork_t_kernel(tc, target_q, target_k, target_v, cond_k, c
         def load(c):
             b0, nb = starts[c], CHUNKS[c]
             q = ld.tile([P, nb, 512], BF16, tag="q")
-            kt = ld.tile([P, nb, 512], BF16, tag="kt")
-            kc = ld.tile([P, nb, 512], BF16, tag="kc")
+            kt = ld.tile([P, 2 * nb, 256], BF16, tag="kt")
+            kc = ld.tile([P, 2 * nb, 256], BF16, tag="kc")
             v = ld.tile([P, 2 * nb, 512], BF16, tag="v")
             nc.sync.dma_start(out=q[:], in_=target_q[b0:b0 + nb].rearrange("b (r j) h d -> r b (j h d)", j=2))
-            nc.sync.dma_start(out=kt[:], in_=target_k[b0:b0 + nb].rearrange("b (r j) h d -> r b (j h d)", j=2))
-            nc.sync.dma_start(out=kc[:], in_=cond_k[b0:b0 + nb].rearrange("b (r j) h d -> r b (j h d)", j=2))
-            nc.sync.dma_start(out=v[0:64], in_=target_v[b0:b0 + nb].rearrange("b (g r j) h d -> r (b g) (j h d)", g=2, j=2))
-            nc.sync.dma_start(out=v[64:128], in_=cond_v[b0:b0 + nb].rearrange("b (g r j) h d -> r (b g) (j h d)", g=2, j=2))
+            nc.sync.dma_start(out=kt[:], in_=target_k[b0:b0 + nb].rearrange("b (k r) h d -> r (b k) (h d)", k=2))
+            nc.sync.dma_start(out=kc[:], in_=cond_k[b0:b0 + nb].rearrange("b (k r) h d -> r (b k) (h d)", k=2))
+            nc.sync.dma_start(out=v[0:64], in_=target_v[b0:b0 + nb].rearrange("b (u r w) h d -> r (b u) (w h d)", u=2, w=2))
+            nc.sync.dma_start(out=v[64:128], in_=cond_v[b0:b0 + nb].rearrange("b (u r w) h d -> r (b u) (w h d)", u=2, w=2))
             loaded[c] = (q, kt, kc, v)
 
         b_bf = const.tile([P, 1], BF16)
@@ -89,10 +89,10 @@ def tile_easycontrolnetwork_t_kernel(tc, target_q, target_k, target_v, cond_k, c
             for j in range(2):
                 o = j * 256 + h * 128
                 nc.tensor.transpose(qkt_ps[:, j, :], q[:, bi, o:o + 128], ident[:])
-            for j in range(2):
-                o = j * 256 + h * 128
-                nc.tensor.transpose(qkt_ps[:, 2 + j, :], kt[:, bi, o:o + 128], ident[:])
-                nc.tensor.transpose(qkt_ps[:, 4 + j, :], kc[:, bi, o:o + 128], ident[:])
+            for k in range(2):
+                o = h * 128
+                nc.tensor.transpose(qkt_ps[:, 2 + 2 * k, :], kt[:, 2 * bi + k, o:o + 128], ident[:])
+                nc.tensor.transpose(qkt_ps[:, 3 + 2 * k, :], kc[:, 2 * bi + k, o:o + 128], ident[:])
             st[("qkt_ps", n)] = qkt_ps
 
         def act_qk_copy(n):
@@ -102,14 +102,11 @@ def tile_easycontrolnetwork_t_kernel(tc, target_q, target_k, target_v, cond_k, c
 
         def pe_scores(n, jq):
             qkt = st[("qkt", n)]
-            s_ps = ps_s.tile([P, 2, 2, 2, 64], F32, tag="s")
-            for g in range(2):
-                nc.tensor.matmul(s_ps[:, g, :, 1, :], lhsT=qkt[:, jq, :], rhs=qkt[:, 4:6, 64 * g:64 * g + 64],
-                                 start=True, stop=False)
-                nc.tensor.matmul(s_ps[:, g, :, 1, :], lhsT=bmat[:], rhs=ident32[:].rearrange("p (a c) -> p a c", a=2),
-                                 is_transpose=True, start=False, stop=True)
-                nc.tensor.matmul(s_ps[:, g, :, 0, :], lhsT=qkt[:, jq, :], rhs=qkt[:, 2:4, 64 * g:64 * g + 64],
-                                 start=True, stop=True)
+            s_ps = ps_s.tile([P, 4, P], F32, tag="s")
+            for k in range(2):
+                nc.tensor.matmul(s_ps[:, 1 + 2 * k, :], lhsT=qkt[:, jq, :], rhs=qkt[:, 3 + 2 * k, :], start=True, stop=False)
+                nc.tensor.matmul(s_ps[:, 1 + 2 * k, :], lhsT=bmat[:], rhs=ident32[:], is_transpose=True, start=False, stop=True)
+            nc.tensor.matmul(s_ps[:, 0:4:2, :], lhsT=qkt[:, jq, :], rhs=qkt[:, 2:6:2, :], start=True, stop=True)
             st[("s", n, jq)] = s_ps
 
         def dve_max(n, jq):
@@ -118,7 +115,7 @@ def tile_easycontrolnetwork_t_kernel(tc, target_q, target_k, target_v, cond_k, c
                 st[("mx", n)] = mx
             nc.vector.tensor_reduce(
                 out=st[("mx", n)][:, jq:jq + 1],
-                in_=st[("s", n, jq)][:].rearrange("q g j y p -> q (g j y p)"),
+                in_=st[("s", n, jq)][:].rearrange("q t c -> q (t c)"),
                 axis=AX.X,
                 op=ALU.max,
             )
@@ -138,22 +135,24 @@ def tile_easycontrolnetwork_t_kernel(tc, target_q, target_k, target_v, cond_k, c
             negm = st[("negm", n)]
             for jq in range(2):
                 nc.scalar.activation(out=e[:, jq].rearrange("q t c -> q (t c)"),
-                                     in_=st[("s", n, jq)][:].rearrange("q g j y p -> q (g j y p)"), func=ACTF.Exp,
+                                     in_=st[("s", n, jq)][:].rearrange("q t c -> q (t c)"), func=ACTF.Exp,
                                      bias=negm[:, jq:jq + 1], scale=SCALE, accum_out=rs[:, h, jq:jq + 1])
             st[("e", n)] = e
 
         def pe_e_transposes(n):
             e = st[("e", n)]
-            et_ps = ps_2.tile([P, 2, 4, P], BF16, tag="et")
+            et_ps = ps_2.tile([P, 2, 2, P], F32, tag="et")
             for jq in range(2):
-                for t in range(4):
-                    nc.tensor.transpose(et_ps[:, jq, t, :], e[:, jq, t, :], ident[:])
+                for u in range(2):
+                    nc.tensor.transpose(et_ps[:, jq, u, :],
+                                        e[:, jq, 2 * u:2 * u + 2, :].rearrange("q t c -> q (t c)").bitcast(F32), ident32[:])
             st[("et", n)] = et_ps
 
         def copy_et(n):
             eg = work.tile([P, 2, P, 4], BF16, tag="eg", align_bytes=64)
             st[("eg", n)] = eg
-            nc.scalar.copy(out=eg[:], in_=st[("et", n)][:].rearrange("p a t q -> p a q t"))
+            nc.scalar.copy(out=eg[:].rearrange("p a q t -> p (a q t)").bitcast(F32).rearrange("p (a q u) -> p a q u", a=2, u=2),
+                           in_=st[("et", n)][:].rearrange("p a u q -> p a q u"))
 
         def dve_quant_e(n):
             ec = eqp.tile([P, 2 * P], U32, tag="ec", align_bytes=64)
@@ -167,8 +166,8 @@ def tile_easycontrolnetwork_t_kernel(tc, target_q, target_k, target_v, cond_k, c
             c, bi = where[b]
             v = loaded[c][3]
             vg = vgp.tile([P, P, 4], BF16, tag="vg", align_bytes=64)
-            src = v[:, 2 * bi:2 * bi + 2, :].rearrange("p g (j h d) -> p g j h d", j=2, h=2)[:, :, :, h, :]
-            nc.gpsimd.tensor_scalar(out=vg[:], in0=src.rearrange("p g j d -> p d (g j)"), scalar1=1.0, scalar2=0.0,
+            src = v[:, 2 * bi:2 * bi + 2, :].rearrange("p u (w h d) -> p u w h d", w=2, h=2)[:, :, :, h, :]
+            nc.gpsimd.tensor_scalar(out=vg[:], in0=src.rearrange("p u w d -> p d (u w)"), scalar1=1.0, scalar2=0.0,
                                     op0=ALU.mult, op1=ALU.add)
             st[("vg", n)] = vg
 

@@ -97,7 +97,8 @@ def tile_easycontrolnetwork_t_kernel(tc, target_q, target_k, target_v, cond_k, c
 
         def act_qk_copy(n):
             qkt = work.tile([P, 6, P], BF16, tag="qkt")
-            nc.vector.tensor_copy(out=qkt[:], in_=st[("qkt_ps", n)][:])
+            nc.scalar.copy(out=qkt[:].rearrange("p a c -> p (a c)").bitcast(F32),
+                           in_=st[("qkt_ps", n)][:].rearrange("p a c -> p (a c)").bitcast(F32))
             st[("qkt", n)] = qkt
 
         def pe_scores(n, jq):

@@ -70,8 +70,9 @@ def tile_easycontrolnetwork_t_kernel(tc, target_q, target_k, target_v, cond_k, c
         nc.vector.tensor_scalar(out=bs[:], in0=b_bf[:], scalar1=1.0 / SCALE, scalar2=None, op0=ALU.mult)
         ident32 = const.tile([P, P], F32)
         make_identity(nc, ident32[:])
-        bmat = const.tile([P, P], F32)
-        nc.vector.tensor_copy(out=bmat[:], in_=bs[:, 0:1].to_broadcast([P, P]))
+        b01 = const.tile([P, 2], F32)
+        nc.vector.memset(b01[:, 0:1], 0.0)
+        nc.vector.tensor_copy(out=b01[:, 1:2], in_=b_bf[:])
 
         if PIN:
             ctx.enter_context(tc.manual_schedule())
@@ -91,8 +92,8 @@ def tile_easycontrolnetwork_t_kernel(tc, target_q, target_k, target_v, cond_k, c
                 nc.tensor.transpose(qkt_ps[:, j, :], q[:, bi, o:o + 128], ident[:])
             for k in range(2):
                 o = h * 128
-                nc.tensor.transpose(qkt_ps[:, 2 + 2 * k, :], kt[:, 2 * bi + k, o:o + 128], ident[:])
-                nc.tensor.transpose(qkt_ps[:, 3 + 2 * k, :], kc[:, 2 * bi + k, o:o + 128], ident[:])
+                nc.tensor.transpose(qkt_ps[:, 2 + k, :], kt[:, 2 * bi + k, o:o + 128], ident[:])
+                nc.tensor.transpose(qkt_ps[:, 4 + k, :], kc[:, 2 * bi + k, o:o + 128], ident[:])
             st[("qkt_ps", n)] = qkt_ps
 
         def act_qk_copy(n):
@@ -103,41 +104,48 @@ def tile_easycontrolnetwork_t_kernel(tc, target_q, target_k, target_v, cond_k, c
 
         def pe_scores(n, jq):
             qkt = st[("qkt", n)]
-            s_ps = ps_s.tile([P, 4, P], F32, tag="s")
-            for k in range(2):
-                nc.tensor.matmul(s_ps[:, 1 + 2 * k, :], lhsT=qkt[:, jq, :], rhs=qkt[:, 3 + 2 * k, :], start=True, stop=False)
-                nc.tensor.matmul(s_ps[:, 1 + 2 * k, :], lhsT=bmat[:], rhs=ident32[:], is_transpose=True, start=False, stop=True)
-            nc.tensor.matmul(s_ps[:, 0:4:2, :], lhsT=qkt[:, jq, :], rhs=qkt[:, 2:6:2, :], start=True, stop=True)
+            s_ps = ps_s.tile([P, 2, 2, P], F32, tag="s")
+            nc.tensor.matmul(s_ps[:].rearrange("q y u c -> q (y u c)"), lhsT=qkt[:, jq, :],
+                             rhs=qkt[:, 2:6, :].rearrange("d a c -> d (a c)"), start=True, stop=True)
             st[("s", n, jq)] = s_ps
 
         def dve_max(n, jq):
             if jq == 0:
-                mx = small.tile([P, 2], F32, tag="mx")
+                mx = small.tile([P, 2, 2], F32, tag="mx")
                 st[("mx", n)] = mx
             nc.vector.tensor_reduce(
-                out=st[("mx", n)][:, jq:jq + 1],
-                in_=st[("s", n, jq)][:].rearrange("q t c -> q (t c)"),
+                out=st[("mx", n)][:, jq, :],
+                in_=st[("s", n, jq)][:].rearrange("q y u c -> q y (u c)"),
                 axis=AX.X,
                 op=ALU.max,
             )
 
+        def dve_comb(n):
+            m = small.tile([P, 2], F32, tag="m")
+            mx = st[("mx", n)]
+            nc.vector.scalar_tensor_tensor(out=m[:], in0=mx[:, :, 1], scalar=bs[:, 0:1], in1=mx[:, :, 0],
+                                           op0=ALU.add, op1=ALU.max)
+            st[("m", n)] = m
+
         def dve_bias(n):
-            negm = small.tile([P, 2], F32, tag="negm")
-            nc.vector.tensor_scalar(out=negm[:], in0=st[("mx", n)][:], scalar1=-SCALE, scalar2=None, op0=ALU.mult)
+            negm = small.tile([P, 2, 2], F32, tag="negm")
+            nc.vector.scalar_tensor_tensor(out=negm[:], in0=st[("m", n)][:].unsqueeze(1).to_broadcast([P, 2, 2]),
+                                           scalar=-SCALE, in1=b01[:].unsqueeze(2).to_broadcast([P, 2, 2]),
+                                           op0=ALU.mult, op1=ALU.add)
             st[("negm", n)] = negm
 
         def act_exp(n):
             b, h = divmod(n, 2)
             e = work.tile([P, 2, 4, P], BF16, tag="e")
             if h == 0:
-                rs = small.tile([P, 2, 2], F32, tag="rs")
+                rs = small.tile([P, 2, 2, 2], F32, tag="rs")
                 st[("rs", b)] = rs
             rs = st[("rs", b)]
             negm = st[("negm", n)]
             for jq in range(2):
-                nc.scalar.activation(out=e[:, jq].rearrange("q t c -> q (t c)"),
-                                     in_=st[("s", n, jq)][:].rearrange("q t c -> q (t c)"), func=ACTF.Exp,
-                                     bias=negm[:, jq:jq + 1], scale=SCALE, accum_out=rs[:, h, jq:jq + 1])
+                for y in range(2):
+                    nc.scalar.activation(out=e[:, jq, y:4:2, :], in_=st[("s", n, jq)][:, y, :, :], func=ACTF.Exp,
+                                         bias=negm[:, y, jq:jq + 1], scale=SCALE, accum_out=rs[:, h, jq, y:y + 1])
             st[("e", n)] = e
 
         def pe_e_transposes(n):
@@ -195,9 +203,14 @@ def tile_easycontrolnetwork_t_kernel(tc, target_q, target_k, target_v, cond_k, c
                 )
             st[("o", n)] = o_ps
 
+        def dve_rsum(b):
+            rsum = small.tile([P, 2, 2], F32, tag="rsum")
+            nc.vector.tensor_reduce(out=rsum[:], in_=st[("rs", b)][:], axis=AX.X, op=ALU.add)
+            st[("rsum", b)] = rsum
+
         def dve_rinv(b):
             rinv = small.tile([P, 2, 2], F32, tag="rinv")
-            nc.vector.reciprocal(out=rinv[:], in_=st[("rs", b)][:])
+            nc.vector.reciprocal(out=rinv[:], in_=st[("rsum", b)][:])
             st[("rinv", b)] = rinv
 
         def norm(n):
@@ -239,9 +252,13 @@ def tile_easycontrolnetwork_t_kernel(tc, target_q, target_k, target_v, cond_k, c
             if ok(i - 7):
                 norm(i - 7)
             if ok(i):
-                dve_bias(i)
+                dve_comb(i)
+            if i % 2 == 0 and 0 <= (i - 4) // 2 < B:
+                dve_rsum((i - 4) // 2)
             if ok(i - 5):
                 dve_quant_e(i - 5)
+            if ok(i):
+                dve_bias(i)
             if i % 2 == 0 and 0 <= (i - 4) // 2 < B:
                 dve_rinv((i - 4) // 2)
             if ok(i):

@@ -187,21 +187,22 @@ def tile_easycontrolnetwork_t_kernel(tc, target_q, target_k, target_v, cond_k, c
                                   in_=st[("vg", n)][:].rearrange("p c t -> p (c t)"))
             st[("vc", n)] = (vc, vs)
 
-        def pe_pv(n):
-            ec, es = st[("ec", n)]
-            vc, vs = st[("vc", n)]
-            o_ps = ps_1.tile([P, 2, P], F32, tag="o_ps")
-            for jq in range(2):
-                nc.tensor.matmul_mx(
-                    out=o_ps[:, jq, :],
-                    lhsT=ec[:, 128 * jq:128 * jq + 128].bitcast(FP8X4),
-                    lhsT_scale=es[:, 128 * jq:128 * jq + 128],
-                    rhs=vc[:].bitcast(FP8X4),
-                    rhs_scale=vs[:],
-                    start=True,
-                    stop=True,
-                )
-            st[("o", n)] = o_ps
+        def pe_pv(b):
+            o_ps = ps_1.tile([P, 2, 2, P], F32, tag="o_ps")
+            for h in range(2):
+                ec, es = st[("ec", 2 * b + h)]
+                vc, vs = st[("vc", 2 * b + h)]
+                for jq in range(2):
+                    nc.tensor.matmul_mx(
+                        out=o_ps[:, jq, h, :],
+                        lhsT=ec[:, 128 * jq:128 * jq + 128].bitcast(FP8X4),
+                        lhsT_scale=es[:, 128 * jq:128 * jq + 128],
+                        rhs=vc[:].bitcast(FP8X4),
+                        rhs_scale=vs[:],
+                        start=True,
+                        stop=True,
+                    )
+            st[("o", b)] = o_ps
 
         def dve_rsum(b):
             rsum = small.tile([P, 2, 2], F32, tag="rsum")
@@ -213,17 +214,13 @@ def tile_easycontrolnetwork_t_kernel(tc, target_q, target_k, target_v, cond_k, c
             nc.vector.reciprocal(out=rinv[:], in_=st[("rsum", b)][:])
             st[("rinv", b)] = rinv
 
-        def norm(n):
-            b, h = divmod(n, 2)
-            if h == 0:
-                osb = work.tile([P, 2, 2 * P], F32, tag="osb")
-                st[("osb", b)] = osb
-            osb = st[("osb", b)]
-            nc.vector.tensor_tensor(out=osb[:, :, 128 * h:128 * h + 128], in0=st[("o", n)][:],
-                                    in1=st[("rinv", b)][:, h, :].unsqueeze(2).to_broadcast([P, 2, P]), op=ALU.mult)
-            if h == 1:
-                nc.sync.dma_start(out=out[b].rearrange("(r j) c -> r (j c)", j=2),
-                                  in_=osb[:].rearrange("p j c -> p (j c)"))
+        def norm(b):
+            osb = work.tile([P, 2, 2, P], F32, tag="osb")
+            nc.vector.tensor_tensor(out=osb[:], in0=st[("o", b)][:],
+                                    in1=st[("rinv", b)][:].rearrange("p h j -> p j h").unsqueeze(3).to_broadcast([P, 2, 2, P]),
+                                    op=ALU.mult)
+            nc.sync.dma_start(out=out[b].rearrange("(r j) c -> r (j c)", j=2),
+                              in_=osb[:].rearrange("p j h d -> p (j h d)"))
 
         last_head = {}
         for c, nb in enumerate(CHUNKS):
@@ -238,20 +235,20 @@ def tile_easycontrolnetwork_t_kernel(tc, target_q, target_k, target_v, cond_k, c
                 act_qk_copy(i + 1)
             if ok(i):
                 pe_scores(i, 0)
-            if ok(i - 7):
-                pe_pv(i - 7)
+            if i % 2 == 0 and 0 <= (i - 8) // 2 < B:
+                pe_pv((i - 8) // 2)
             if ok(i):
                 pe_scores(i, 1)
             if ok(i - 3):
                 pe_e_transposes(i - 3)
             if ok(i + 2):
                 pe_qk_transposes(i + 2)
+            if i % 2 == 1 and 0 <= (i - 9) // 2 < B:
+                norm((i - 9) // 2)
             if ok(i):
                 dve_max(i, 0)
                 dve_max(i, 1)
-            if ok(i - 7):
-                norm(i - 7)
-            if ok(i):
+                dve_quant_v(i)
                 dve_comb(i)
             if i % 2 == 0 and 0 <= (i - 4) // 2 < B:
                 dve_rsum((i - 4) // 2)
@@ -261,8 +258,6 @@ def tile_easycontrolnetwork_t_kernel(tc, target_q, target_k, target_v, cond_k, c
                 dve_bias(i)
             if i % 2 == 0 and 0 <= (i - 4) // 2 < B:
                 dve_rinv((i - 4) // 2)
-            if ok(i):
-                dve_quant_v(i)
             if ok(i + 1):
                 pool_regroup_v(i + 1)
             if (i + 1) in last_head and last_head[i + 1] + LD_BUFS < len(CHUNKS):

@@ -70,9 +70,8 @@ def tile_easycontrolnetwork_t_kernel(tc, target_q, target_k, target_v, cond_k, c
         nc.vector.tensor_scalar(out=bs[:], in0=b_bf[:], scalar1=1.0 / SCALE, scalar2=None, op0=ALU.mult)
         ident32 = const.tile([P, P], F32)
         make_identity(nc, ident32[:])
-        b01 = const.tile([P, 2], F32)
-        nc.vector.memset(b01[:, 0:1], 0.0)
-        nc.vector.tensor_copy(out=b01[:, 1:2], in_=b_bf[:])
+        bmat = const.tile([P, P], F32)
+        nc.vector.tensor_copy(out=bmat[:], in_=bs[:, 0:1].to_broadcast([P, P]))
 
         if PIN:
             ctx.enter_context(tc.manual_schedule())
@@ -92,8 +91,8 @@ def tile_easycontrolnetwork_t_kernel(tc, target_q, target_k, target_v, cond_k, c
                 nc.tensor.transpose(qkt_ps[:, j, :], q[:, bi, o:o + 128], ident[:])
             for k in range(2):
                 o = h * 128
-                nc.tensor.transpose(qkt_ps[:, 2 + k, :], kt[:, 2 * bi + k, o:o + 128], ident[:])
-                nc.tensor.transpose(qkt_ps[:, 4 + k, :], kc[:, 2 * bi + k, o:o + 128], ident[:])
+                nc.tensor.transpose(qkt_ps[:, 2 + 2 * k, :], kt[:, 2 * bi + k, o:o + 128], ident[:])
+                nc.tensor.transpose(qkt_ps[:, 3 + 2 * k, :], kc[:, 2 * bi + k, o:o + 128], ident[:])
             st[("qkt_ps", n)] = qkt_ps
 
         def act_qk_copy(n):
@@ -104,48 +103,41 @@ def tile_easycontrolnetwork_t_kernel(tc, target_q, target_k, target_v, cond_k, c
 
         def pe_scores(n, jq):
             qkt = st[("qkt", n)]
-            s_ps = ps_s.tile([P, 2, 2, P], F32, tag="s")
-            nc.tensor.matmul(s_ps[:].rearrange("q y u c -> q (y u c)"), lhsT=qkt[:, jq, :],
-                             rhs=qkt[:, 2:6, :].rearrange("d a c -> d (a c)"), start=True, stop=True)
+            s_ps = ps_s.tile([P, 4, P], F32, tag="s")
+            nc.tensor.matmul(s_ps[:].rearrange("q t c -> q (t c)"), lhsT=qkt[:, jq, :],
+                             rhs=qkt[:, 2:6, :].rearrange("d a c -> d (a c)"), start=True, stop=False)
+            for k in range(2):
+                nc.tensor.matmul(s_ps[:, 1 + 2 * k, :], lhsT=bmat[:], rhs=ident32[:], is_transpose=True, start=False, stop=(k == 1))
             st[("s", n, jq)] = s_ps
 
         def dve_max(n, jq):
             if jq == 0:
-                mx = small.tile([P, 2, 2], F32, tag="mx")
+                mx = small.tile([P, 2], F32, tag="mx")
                 st[("mx", n)] = mx
             nc.vector.tensor_reduce(
-                out=st[("mx", n)][:, jq, :],
-                in_=st[("s", n, jq)][:].rearrange("q y u c -> q y (u c)"),
+                out=st[("mx", n)][:, jq:jq + 1],
+                in_=st[("s", n, jq)][:].rearrange("q t c -> q (t c)"),
                 axis=AX.X,
                 op=ALU.max,
             )
 
-        def dve_comb(n):
-            m = small.tile([P, 2], F32, tag="m")
-            mx = st[("mx", n)]
-            nc.vector.scalar_tensor_tensor(out=m[:], in0=mx[:, :, 1], scalar=bs[:, 0:1], in1=mx[:, :, 0],
-                                           op0=ALU.add, op1=ALU.max)
-            st[("m", n)] = m
-
         def dve_bias(n):
-            negm = small.tile([P, 2, 2], F32, tag="negm")
-            nc.vector.scalar_tensor_tensor(out=negm[:], in0=st[("m", n)][:].unsqueeze(1).to_broadcast([P, 2, 2]),
-                                           scalar=-SCALE, in1=b01[:].unsqueeze(2).to_broadcast([P, 2, 2]),
-                                           op0=ALU.mult, op1=ALU.add)
+            negm = small.tile([P, 2], F32, tag="negm")
+            nc.vector.tensor_scalar(out=negm[:], in0=st[("mx", n)][:], scalar1=-SCALE, scalar2=None, op0=ALU.mult)
             st[("negm", n)] = negm
 
         def act_exp(n):
             b, h = divmod(n, 2)
             e = work.tile([P, 2, 4, P], BF16, tag="e")
             if h == 0:
-                rs = small.tile([P, 2, 2, 2], F32, tag="rs")
+                rs = small.tile([P, 2, 2], F32, tag="rs")
                 st[("rs", b)] = rs
             rs = st[("rs", b)]
             negm = st[("negm", n)]
             for jq in range(2):
-                for y in range(2):
-                    nc.scalar.activation(out=e[:, jq, y:4:2, :], in_=st[("s", n, jq)][:, y, :, :], func=ACTF.Exp,
-                                         bias=negm[:, y, jq:jq + 1], scale=SCALE, accum_out=rs[:, h, jq, y:y + 1])
+                nc.scalar.activation(out=e[:, jq].rearrange("q t c -> q (t c)"),
+                                     in_=st[("s", n, jq)][:].rearrange("q t c -> q (t c)"), func=ACTF.Exp,
+                                     bias=negm[:, jq:jq + 1], scale=SCALE, accum_out=rs[:, h, jq:jq + 1])
             st[("e", n)] = e
 
         def pe_e_transposes(n):
@@ -204,14 +196,9 @@ def tile_easycontrolnetwork_t_kernel(tc, target_q, target_k, target_v, cond_k, c
                     )
             st[("o", b)] = o_ps
 
-        def dve_rsum(b):
-            rsum = small.tile([P, 2, 2], F32, tag="rsum")
-            nc.vector.tensor_reduce(out=rsum[:], in_=st[("rs", b)][:], axis=AX.X, op=ALU.add)
-            st[("rsum", b)] = rsum
-
         def dve_rinv(b):
             rinv = small.tile([P, 2, 2], F32, tag="rinv")
-            nc.vector.reciprocal(out=rinv[:], in_=st[("rsum", b)][:])
+            nc.vector.reciprocal(out=rinv[:], in_=st[("rs", b)][:])
             st[("rinv", b)] = rinv
 
         def norm(b):
@@ -249,13 +236,9 @@ def tile_easycontrolnetwork_t_kernel(tc, target_q, target_k, target_v, cond_k, c
                 dve_max(i, 0)
                 dve_max(i, 1)
                 dve_quant_v(i)
-                dve_comb(i)
-            if i % 2 == 0 and 0 <= (i - 4) // 2 < B:
-                dve_rsum((i - 4) // 2)
+                dve_bias(i)
             if ok(i - 5):
                 dve_quant_e(i - 5)
-            if ok(i):
-                dve_bias(i)
             if i % 2 == 0 and 0 <= (i - 4) // 2 < B:
                 dve_rinv((i - 4) // 2)
             if ok(i + 1):

@@ -18,7 +18,7 @@ NHEADS = B * H
 SCALE = D ** -0.5
 FLOPS = 2 * 2 * B * H * S * (2 * S) * D
 
-CHUNKS = [1, 1, 2, 4, 4, 4, 4, 4, 4, 4]
+CHUNKS = [1, 1] + [2] * 15
 LD_BUFS = 4
 PIN = True
 
@@ -36,6 +36,7 @@ def tile_easycontrolnetwork_t_kernel(tc, target_q, target_k, target_v, cond_k, c
         const = ctx.enter_context(tc.tile_pool(name="const", bufs=1))
         ld = ctx.enter_context(tc.tile_pool(name="ld", bufs=LD_BUFS))
         work = ctx.enter_context(tc.tile_pool(name="work", bufs=3))
+        outp = ctx.enter_context(tc.tile_pool(name="outp", bufs=4))
         small = ctx.enter_context(tc.tile_pool(name="small", bufs=4))
         vgp = ctx.enter_context(tc.tile_pool(name="vgp", bufs=2))
         vqp = ctx.enter_context(tc.tile_pool(name="vqp", bufs=10))
@@ -202,7 +203,7 @@ def tile_easycontrolnetwork_t_kernel(tc, target_q, target_k, target_v, cond_k, c
             st[("rinv", b)] = rinv
 
         def norm(b):
-            osb = work.tile([P, 2, 2, P], F32, tag="osb")
+            osb = outp.tile([P, 2, 2, P], F32, tag="osb")
             nc.vector.tensor_tensor(out=osb[:], in0=st[("o", b)][:],
                                     in1=st[("rinv", b)][:].rearrange("p h j -> p j h").unsqueeze(3).to_broadcast([P, 2, 2, P]),
                                     op=ALU.mult)

@@ -50,14 +50,14 @@ def tile_easycontrolnetwork_t_kernel(tc, target_q, target_k, target_v, cond_k, c
         def load(c):
             b0, nb = starts[c], CHUNKS[c]
             q = ld.tile([P, nb, 512], BF16, tag="q")
-            kt = ld.tile([P, 2 * nb, 256], BF16, tag="kt")
-            kc = ld.tile([P, 2 * nb, 256], BF16, tag="kc")
-            v = ld.tile([P, 2 * nb, 512], BF16, tag="v")
+            kt = ld.tile([P, nb, 512], BF16, tag="kt")
+            kc = ld.tile([P, nb, 512], BF16, tag="kc")
+            v = ld.tile([P, nb, 1024], BF16, tag="v")
             nc.sync.dma_start(out=q[:], in_=target_q[b0:b0 + nb].rearrange("b (r j) h d -> r b (j h d)", j=2))
-            nc.sync.dma_start(out=kt[:], in_=target_k[b0:b0 + nb].rearrange("b (k r) h d -> r (b k) (h d)", k=2))
-            nc.sync.dma_start(out=kc[:], in_=cond_k[b0:b0 + nb].rearrange("b (k r) h d -> r (b k) (h d)", k=2))
-            nc.sync.dma_start(out=v[0:64], in_=target_v[b0:b0 + nb].rearrange("b (u r w) h d -> r (b u) (w h d)", u=2, w=2))
-            nc.sync.dma_start(out=v[64:128], in_=cond_v[b0:b0 + nb].rearrange("b (u r w) h d -> r (b u) (w h d)", u=2, w=2))
+            nc.sync.dma_start(out=kt[:], in_=target_k[b0:b0 + nb].rearrange("b (r k) h d -> r b (k h d)", k=2))
+            nc.sync.dma_start(out=kc[:], in_=cond_k[b0:b0 + nb].rearrange("b (r k) h d -> r b (k h d)", k=2))
+            nc.sync.dma_start(out=v[0:64], in_=target_v[b0:b0 + nb].rearrange("b (r o) h d -> r b (o h d)", o=4))
+            nc.sync.dma_start(out=v[64:128], in_=cond_v[b0:b0 + nb].rearrange("b (r o) h d -> r b (o h d)", o=4))
             loaded[c] = (q, kt, kc, v)
 
         b_bf = const.tile([P, 1], BF16)
@@ -91,9 +91,9 @@ def tile_easycontrolnetwork_t_kernel(tc, target_q, target_k, target_v, cond_k, c
                 o = j * 256 + h * 128
                 nc.tensor.transpose(qkt_ps[:, j, :], q[:, bi, o:o + 128], ident[:])
             for k in range(2):
-                o = h * 128
-                nc.tensor.transpose(qkt_ps[:, 2 + 2 * k, :], kt[:, 2 * bi + k, o:o + 128], ident[:])
-                nc.tensor.transpose(qkt_ps[:, 3 + 2 * k, :], kc[:, 2 * bi + k, o:o + 128], ident[:])
+                o = k * 256 + h * 128
+                nc.tensor.transpose(qkt_ps[:, 2 + 2 * k, :], kt[:, bi, o:o + 128], ident[:])
+                nc.tensor.transpose(qkt_ps[:, 3 + 2 * k, :], kc[:, bi, o:o + 128], ident[:])
             st[("qkt_ps", n)] = qkt_ps
 
         def act_qk_copy(n):
@@ -168,8 +168,8 @@ def tile_easycontrolnetwork_t_kernel(tc, target_q, target_k, target_v, cond_k, c
             c, bi = where[b]
             v = loaded[c][3]
             vg = vgp.tile([P, P, 4], BF16, tag="vg", align_bytes=64)
-            src = v[:, 2 * bi:2 * bi + 2, :].rearrange("p u (w h d) -> p u w h d", w=2, h=2)[:, :, :, h, :]
-            nc.gpsimd.tensor_scalar(out=vg[:], in0=src.rearrange("p u w d -> p d (u w)"), scalar1=1.0, scalar2=0.0,
+            src = v[:, bi, :].rearrange("p (w u h d) -> p w u h d", w=2, u=2, h=2)[:, :, :, h, :]
+            nc.gpsimd.tensor_scalar(out=vg[:].rearrange("p d (u w) -> p d u w", u=2), in0=src.rearrange("p w u d -> p d u w"), scalar1=1.0, scalar2=0.0,
                                     op0=ALU.mult, op1=ALU.add)
             st[("vg", n)] = vg
 

@@ -42,6 +42,7 @@ def tile_easycontrolnetwork_t_kernel(tc, target_q, target_k, target_v, cond_k, c
         vqp = ctx.enter_context(tc.tile_pool(name="vqp", bufs=10))
         eqp = ctx.enter_context(tc.tile_pool(name="eqp", bufs=4))
         ps_s = ctx.enter_context(tc.psum_pool(name="ps_s", bufs=4))
+        ps_q = ctx.enter_context(tc.psum_pool(name="ps_q", bufs=1))
         ps_1 = ctx.enter_context(tc.psum_pool(name="ps_1", bufs=1))
         ps_2 = ctx.enter_context(tc.psum_pool(name="ps_2", bufs=2))
 
@@ -86,7 +87,7 @@ def tile_easycontrolnetwork_t_kernel(tc, target_q, target_k, target_v, cond_k, c
             b, h = divmod(n, 2)
             c, bi = where[b]
             q, kt, kc, v = loaded[c]
-            qkt_ps = ps_1.tile([P, 6, P], BF16, tag="qkt_ps")
+            qkt_ps = ps_q.tile([P, 6, P], BF16, tag="qkt_ps")
             for j in range(2):
                 o = j * 256 + h * 128
                 nc.tensor.transpose(qkt_ps[:, j, :], q[:, bi, o:o + 128], ident[:])
@@ -95,6 +96,11 @@ def tile_easycontrolnetwork_t_kernel(tc, target_q, target_k, target_v, cond_k, c
                 nc.tensor.transpose(qkt_ps[:, 2 + 2 * k, :], kt[:, bi, o:o + 128], ident[:])
                 nc.tensor.transpose(qkt_ps[:, 3 + 2 * k, :], kc[:, bi, o:o + 128], ident[:])
             st[("qkt_ps", n)] = qkt_ps
+
+        def dve_qk_copy(n):
+            qkt = work.tile([P, 6, P], BF16, tag="qkt")
+            nc.vector.tensor_copy(out=qkt[:], in_=st[("qkt_ps", n)][:])
+            st[("qkt", n)] = qkt
 
         def act_qk_copy(n):
             qkt = work.tile([P, 6, P], BF16, tag="qkt")
@@ -214,12 +220,14 @@ def tile_easycontrolnetwork_t_kernel(tc, target_q, target_k, target_v, cond_k, c
         for c, nb in enumerate(CHUNKS):
             last_head[2 * (starts[c] + nb) - 1] = c
 
-        for i in range(-2, NHEADS + 8):
+        for i in range(-2, NHEADS + 12):
+            if ok(i + 1) and (i + 1) % 4 == 1:
+                dve_qk_copy(i + 1)
             if ok(i - 2):
                 act_exp(i - 2)
             if ok(i - 4):
                 copy_et(i - 4)
-            if ok(i + 1):
+            if ok(i + 1) and not ((i + 1) % 4 == 1):
                 act_qk_copy(i + 1)
             if ok(i):
                 pe_scores(i, 0)

@@ -88,13 +88,14 @@ def tile_easycontrolnetwork_t_kernel(tc, target_q, target_k, target_v, cond_k, c
             c, bi = where[b]
             q, kt, kc, v = loaded[c]
             qkt_ps = ps_q.tile([P, 6, P], BF16, tag="qkt_ps")
-            for j in range(2):
-                o = j * 256 + h * 128
-                nc.tensor.transpose(qkt_ps[:, j, :], q[:, bi, o:o + 128], ident[:])
-            for k in range(2):
-                o = k * 256 + h * 128
-                nc.tensor.transpose(qkt_ps[:, 2 + 2 * k, :], kt[:, bi, o:o + 128], ident[:])
-                nc.tensor.transpose(qkt_ps[:, 3 + 2 * k, :], kc[:, bi, o:o + 128], ident[:])
+            parts = [(q, 0), (q, 1), (kt, 0), (kc, 0), (kt, 1), (kc, 1)]
+            for s in range(6):
+                src, j = parts[s]
+                rows = src[:, bi, j * 256 + h * 128:j * 256 + h * 128 + 128]
+                if s < (6 if n < 3 else n % 2):
+                    nc.tensor.matmul(qkt_ps[:, s, :], lhsT=rows, rhs=ident[:], start=True, stop=True)
+                else:
+                    nc.tensor.transpose(qkt_ps[:, s, :], rows, ident[:])
             st[("qkt_ps", n)] = qkt_ps
 
         def dve_qk_copy(n):

@@ -232,7 +232,7 @@ def tile_easycontrolnetwork_t_kernel(tc, target_q, target_k, target_v, cond_k, c
                 act_qk_copy(i + 1)
             if ok(i):
                 pe_scores(i, 0)
-            if i % 2 == 0 and 0 <= (i - 8) // 2 < B:
+            if (i - 8) % 2 == 0 and 0 <= (i - 8) // 2 < B:
                 pe_pv((i - 8) // 2)
             if ok(i):
                 pe_scores(i, 1)
@@ -240,15 +240,18 @@ def tile_easycontrolnetwork_t_kernel(tc, target_q, target_k, target_v, cond_k, c
                 pe_e_transposes(i - 3)
             if ok(i + 2):
                 pe_qk_transposes(i + 2)
-            if i % 2 == 1 and 0 <= (i - 9) // 2 < B:
+            if (i - 9) % 2 == 0 and 0 <= (i - 9) // 2 < B:
                 norm((i - 9) // 2)
             if ok(i):
                 dve_max(i, 0)
+            if ok(i):
                 dve_max(i, 1)
-                dve_quant_v(i)
-                dve_bias(i)
             if ok(i - 5):
                 dve_quant_e(i - 5)
+            if ok(i):
+                dve_bias(i)
+            if ok(i):
+                dve_quant_v(i)
             if i % 2 == 0 and 0 <= (i - 4) // 2 < B:
                 dve_rinv((i - 4) // 2)
             if ok(i + 1):

@@ -21,6 +21,7 @@ FLOPS = 2 * 2 * B * H * S * (2 * S) * D
 CHUNKS = [1, 1] + [2] * 15
 LD_BUFS = 4
 PIN = True
+BOTH = (0, 1)
 
 
 def tile_easycontrolnetwork_t_kernel(tc, target_q, target_k, target_v, cond_k, cond_v, b_param, out):
@@ -36,7 +37,7 @@ def tile_easycontrolnetwork_t_kernel(tc, target_q, target_k, target_v, cond_k, c
         const = ctx.enter_context(tc.tile_pool(name="const", bufs=1))
         ld = ctx.enter_context(tc.tile_pool(name="ld", bufs=LD_BUFS))
         work = ctx.enter_context(tc.tile_pool(name="work", bufs=3))
-        outp = ctx.enter_context(tc.tile_pool(name="outp", bufs=4))
+        outp = ctx.enter_context(tc.tile_pool(name="outp", bufs=6))
         small = ctx.enter_context(tc.tile_pool(name="small", bufs=4))
         vgp = ctx.enter_context(tc.tile_pool(name="vgp", bufs=2))
         vqp = ctx.enter_context(tc.tile_pool(name="vqp", bufs=10))
@@ -66,6 +67,10 @@ def tile_easycontrolnetwork_t_kernel(tc, target_q, target_k, target_v, cond_k, c
         for c in range(LD_BUFS):
             load(c)
 
+        zero = const.tile([P, 1], F32)
+        nc.vector.memset(zero[:], 0.0)
+        exp_zero = const.tile([P, 1], F32)
+        nc.scalar.activation(out=exp_zero[:], in_=zero[:], func=ACTF.Exp)
         ident = const.tile([P, P], BF16)
         make_identity(nc, ident[:])
         bs = const.tile([P, 1], F32)
@@ -92,7 +97,7 @@ def tile_easycontrolnetwork_t_kernel(tc, target_q, target_k, target_v, cond_k, c
             for s in range(6):
                 src, j = parts[s]
                 rows = src[:, bi, j * 256 + h * 128:j * 256 + h * 128 + 128]
-                if s < (6 if n < 3 else n % 2):
+                if s < (6 if n < 3 else (n + 1) % 2):
                     nc.tensor.matmul(qkt_ps[:, s, :], lhsT=rows, rhs=ident[:], start=True, stop=True)
                 else:
                     nc.tensor.transpose(qkt_ps[:, s, :], rows, ident[:])
@@ -134,41 +139,44 @@ def tile_easycontrolnetwork_t_kernel(tc, target_q, target_k, target_v, cond_k, c
             nc.vector.tensor_scalar(out=negm[:], in0=st[("mx", n)][:], scalar1=-SCALE, scalar2=None, op0=ALU.mult)
             st[("negm", n)] = negm
 
-        def act_exp(n):
+        def act_exp(n, jq):
             b, h = divmod(n, 2)
-            e = work.tile([P, 2, 4, P], BF16, tag="e")
-            if h == 0:
-                rs = small.tile([P, 2, 2], F32, tag="rs")
-                st[("rs", b)] = rs
-            rs = st[("rs", b)]
-            negm = st[("negm", n)]
-            for jq in range(2):
-                nc.scalar.activation(out=e[:, jq].rearrange("q t c -> q (t c)"),
-                                     in_=st[("s", n, jq)][:].rearrange("q t c -> q (t c)"), func=ACTF.Exp,
-                                     bias=negm[:, jq:jq + 1], scale=SCALE, accum_out=rs[:, h, jq:jq + 1])
-            st[("e", n)] = e
+            if jq == 0:
+                e_new = work.tile([P, 2, 4, P], BF16, tag="e")
+                st[("e", n)] = e_new
+                if h == 0:
+                    rs_new = small.tile([P, 2, 2], F32, tag="rs")
+                    st[("rs", b)] = rs_new
+            nc.scalar.activation(out=st[("e", n)][:, jq].rearrange("q t c -> q (t c)"),
+                                 in_=st[("s", n, jq)][:].rearrange("q t c -> q (t c)"), func=ACTF.Exp,
+                                 bias=st[("negm", n)][:, jq:jq + 1], scale=SCALE, accum_out=st[("rs", b)][:, h, jq:jq + 1])
 
-        def pe_e_transposes(n):
+        def pe_e_transposes(n, jqs, pool, tag):
             e = st[("e", n)]
-            et_ps = ps_2.tile([P, 2, 2, P], F32, tag="et")
-            for jq in range(2):
+            et_ps = pool.tile([P, 2, 2, P], F32, tag=tag)
+            for jq in jqs:
                 for u in range(2):
                     nc.tensor.transpose(et_ps[:, jq, u, :],
                                         e[:, jq, 2 * u:2 * u + 2, :].rearrange("q t c -> q (t c)").bitcast(F32), ident32[:])
-            st[("et", n)] = et_ps
+                st[("et", n, jq)] = et_ps
 
-        def copy_et(n):
-            eg = work.tile([P, 2, P, 4], BF16, tag="eg", align_bytes=64)
-            st[("eg", n)] = eg
-            nc.scalar.copy(out=eg[:].rearrange("p a q t -> p (a q t)").bitcast(F32).rearrange("p (a q u) -> p a q u", a=2, u=2),
-                           in_=st[("et", n)][:].rearrange("p a u q -> p a q u"))
+        def copy_et(n, jqs):
+            m = len(jqs)
+            eg = work.tile([P, m, P, 4], BF16, tag="eg", align_bytes=64)
+            for jq in jqs:
+                st[("eg", n, jq)] = eg
+            words = eg[:].rearrange("p a q t -> p (a q t)").bitcast(F32).rearrange("p (a q u) -> p a q u", a=m, u=2)
+            pairs = st[("et", n, jqs[0])][:, jqs[0]:jqs[0] + m].rearrange("p a u q -> p a q u")
+            nc.scalar.copy(out=words, in_=pairs)
 
-        def dve_quant_e(n):
-            ec = eqp.tile([P, 2 * P], U32, tag="ec", align_bytes=64)
-            es = eqp.tile([P, 2 * P], U8, tag="es", align_bytes=64)
+        def dve_quant_e(n, jqs):
+            m = len(jqs)
+            ec = eqp.tile([P, m * P], U32, tag="ec", align_bytes=64)
+            es = eqp.tile([P, m * P], U8, tag="es", align_bytes=64)
             nc.vector.quantize_mx(out=ec[:].bitcast(FP8X4), scales=es[:],
-                                  in_=st[("eg", n)][:].rearrange("p a q t -> p (a q t)"))
-            st[("ec", n)] = (ec, es)
+                                  in_=st[("eg", n, jqs[0])][:].rearrange("p a q t -> p (a q t)"))
+            for a in range(m):
+                st[("ec", n, jqs[a])] = (ec[:, P * a:P * a + P], es[:, P * a:P * a + P])
 
         def pool_regroup_v(n):
             b, h = divmod(n, 2)
@@ -187,16 +195,15 @@ def tile_easycontrolnetwork_t_kernel(tc, target_q, target_k, target_v, cond_k, c
                                   in_=st[("vg", n)][:].rearrange("p c t -> p (c t)"))
             st[("vc", n)] = (vc, vs)
 
-        def pe_pv(b):
-            o_ps = ps_1.tile([P, 2, 2, P], F32, tag="o_ps")
+        def pe_pv(b, jqs, o_ps):
             for h in range(2):
-                ec, es = st[("ec", 2 * b + h)]
                 vc, vs = st[("vc", 2 * b + h)]
-                for jq in range(2):
+                for jq in jqs:
+                    ec, es = st[("ec", 2 * b + h, jq)]
                     nc.tensor.matmul_mx(
                         out=o_ps[:, jq, h, :],
-                        lhsT=ec[:, 128 * jq:128 * jq + 128].bitcast(FP8X4),
-                        lhsT_scale=es[:, 128 * jq:128 * jq + 128],
+                        lhsT=ec.bitcast(FP8X4),
+                        lhsT_scale=es,
                         rhs=vc[:].bitcast(FP8X4),
                         rhs_scale=vs[:],
                         start=True,
@@ -209,48 +216,50 @@ def tile_easycontrolnetwork_t_kernel(tc, target_q, target_k, target_v, cond_k, c
             nc.vector.reciprocal(out=rinv[:], in_=st[("rs", b)][:])
             st[("rinv", b)] = rinv
 
-        def norm(b):
-            osb = outp.tile([P, 2, 2, P], F32, tag="osb")
-            nc.vector.tensor_tensor(out=osb[:], in0=st[("o", b)][:],
-                                    in1=st[("rinv", b)][:].rearrange("p h j -> p j h").unsqueeze(3).to_broadcast([P, 2, 2, P]),
+        def norm(b, jqs):
+            m = len(jqs)
+            j0 = jqs[0]
+            osb = outp.tile([P, m, 2, P], F32, tag="osb")
+            nc.vector.tensor_tensor(out=osb[:], in0=st[("o", b)][:, j0:j0 + m],
+                                    in1=st[("rinv", b)][:, :, j0:j0 + m].rearrange("p h j -> p j h").unsqueeze(3).to_broadcast([P, m, 2, P]),
                                     op=ALU.mult)
-            nc.sync.dma_start(out=out[b].rearrange("(r j) c -> r (j c)", j=2),
-                              in_=osb[:].rearrange("p j h d -> p (j h d)"))
+            nc.sync.dma_start(out=out[b].rearrange("(r j) c -> r j c", j=2)[:, j0:j0 + m],
+                              in_=osb[:].rearrange("p j h d -> p j (h d)"))
 
         last_head = {}
         for c, nb in enumerate(CHUNKS):
             last_head[2 * (starts[c] + nb) - 1] = c
 
-        for i in range(-2, NHEADS + 12):
-            if ok(i + 1) and (i + 1) % 4 == 1:
+        for i in range(-2, NHEADS):
+            if ok(i + 1) and (i + 1) % 4 == 2:
                 dve_qk_copy(i + 1)
             if ok(i - 2):
-                act_exp(i - 2)
-            if ok(i - 4):
-                copy_et(i - 4)
-            if ok(i + 1) and not ((i + 1) % 4 == 1):
+                act_exp(i - 2, 0)
+                act_exp(i - 2, 1)
+            if ok(i - 3):
+                copy_et(i - 3, BOTH)
+            if ok(i + 1) and not ((i + 1) % 4 == 2):
                 act_qk_copy(i + 1)
             if ok(i):
                 pe_scores(i, 0)
-            if (i - 8) % 2 == 0 and 0 <= (i - 8) // 2 < B:
-                pe_pv((i - 8) // 2)
+            if (i - 7) % 2 == 0 and 0 <= (i - 7) // 2 < B:
+                o_ps = ps_1.tile([P, 2, 2, P], F32, tag="o_ps")
+                pe_pv((i - 7) // 2, BOTH, o_ps)
             if ok(i):
                 pe_scores(i, 1)
-            if ok(i - 3):
-                pe_e_transposes(i - 3)
+            if ok(i - 2):
+                pe_e_transposes(i - 2, BOTH, ps_2, "et")
             if ok(i + 2):
                 pe_qk_transposes(i + 2)
-            if (i - 9) % 2 == 0 and 0 <= (i - 9) // 2 < B:
-                norm((i - 9) // 2)
+            if (i - 8) % 2 == 0 and 0 <= (i - 8) // 2 < B:
+                norm((i - 8) // 2, BOTH)
             if ok(i):
                 dve_max(i, 0)
-            if ok(i):
                 dve_max(i, 1)
-            if ok(i - 5):
-                dve_quant_e(i - 5)
+            if ok(i - 4):
+                dve_quant_e(i - 4, BOTH)
             if ok(i):
                 dve_bias(i)
-            if ok(i):
                 dve_quant_v(i)
             if i % 2 == 0 and 0 <= (i - 4) // 2 < B:
                 dve_rinv((i - 4) // 2)
@@ -258,3 +267,36 @@ def tile_easycontrolnetwork_t_kernel(tc, target_q, target_k, target_v, cond_k, c
                 pool_regroup_v(i + 1)
             if (i + 1) in last_head and last_head[i + 1] + LD_BUFS < len(CHUNKS):
                 load(last_head[i + 1] + LD_BUFS)
+
+        n = NHEADS - 1
+        b = B - 1
+        act_exp(n - 1, 0)
+        act_exp(n - 1, 1)
+        dve_rinv(b - 1)
+        copy_et(n - 2, BOTH)
+        act_exp(n, 0)
+        act_exp(n, 1)
+        dve_quant_e(n - 3, BOTH)
+        norm(b - 3, BOTH)
+        pe_e_transposes(n - 1, BOTH, ps_2, "et")
+        dve_quant_e(n - 2, BOTH)
+        o_ps = ps_s.tile([P, 2, 2, P], F32, tag="s")
+        pe_pv(b - 2, BOTH, o_ps)
+        pe_e_transposes(n, (0,), ps_2, "et")
+        copy_et(n - 1, BOTH)
+        norm(b - 2, BOTH)
+        o_ps = ps_s.tile([P, 2, 2, P], F32, tag="s")
+        pe_pv(b - 1, BOTH, o_ps)
+        copy_et(n, (0,))
+        pe_e_transposes(n, (1,), ps_s, "s")
+        copy_et(n, (1,))
+        dve_quant_e(n - 1, BOTH)
+        dve_rinv(b)
+        dve_quant_e(n, (0,))
+        dve_quant_e(n, (1,))
+        norm(b - 1, BOTH)
+        o_ps = ps_s.tile([P, 2, 2, P], F32, tag="s")
+        pe_pv(b, (0,), o_ps)
+        pe_pv(b, (1,), o_ps)
+        norm(b, (0,))
+        norm(b, (1,))

@@ -62,8 +62,9 @@ def tile_easycontrolnetwork_t_kernel(tc, target_q, target_k, target_v, cond_k, c
             nc.sync.dma_start(out=v[64:128], in_=cond_v[b0:b0 + nb].rearrange("b (r o) h d -> r b (o h d)", o=4))
             loaded[c] = (q, kt, kc, v)
 
-        b_bf = const.tile([P, 1], BF16)
-        nc.scalar.dma_start(out=b_bf[:], in_=b_param.partition_broadcast(P))
+        b_col = const.tile([P, 1], BF16)
+        nc.vector.memset(b_col[:], 0.0)
+        nc.scalar.dma_start(out=b_col[0:1, :], in_=b_param.partition_broadcast(1))
         for c in range(LD_BUFS):
             load(c)
 
@@ -71,14 +72,13 @@ def tile_easycontrolnetwork_t_kernel(tc, target_q, target_k, target_v, cond_k, c
         nc.vector.memset(zero[:], 0.0)
         exp_zero = const.tile([P, 1], F32)
         nc.scalar.activation(out=exp_zero[:], in_=zero[:], func=ACTF.Exp)
-        ident = const.tile([P, P], BF16)
-        make_identity(nc, ident[:])
-        bs = const.tile([P, 1], F32)
-        nc.vector.tensor_scalar(out=bs[:], in0=b_bf[:], scalar1=1.0 / SCALE, scalar2=None, op0=ALU.mult)
         ident32 = const.tile([P, P], F32)
         make_identity(nc, ident32[:])
+        ident = const.tile([P, P], BF16)
+        make_identity(nc, ident[:])
+        ones = const.tile([P, P], BF16)
+        nc.vector.memset(ones[:], 1.0)
         bmat = const.tile([P, P], F32)
-        nc.vector.tensor_copy(out=bmat[:], in_=bs[:, 0:1].to_broadcast([P, P]))
 
         if PIN:
             ctx.enter_context(tc.manual_schedule())
@@ -97,7 +97,7 @@ def tile_easycontrolnetwork_t_kernel(tc, target_q, target_k, target_v, cond_k, c
             for s in range(6):
                 src, j = parts[s]
                 rows = src[:, bi, j * 256 + h * 128:j * 256 + h * 128 + 128]
-                if s < (6 if n < 3 else (n + 1) % 2):
+                if s < (6 if n < 2 else (n + 1) % 2):
                     nc.tensor.matmul(qkt_ps[:, s, :], lhsT=rows, rhs=ident[:], start=True, stop=True)
                 else:
                     nc.tensor.transpose(qkt_ps[:, s, :], rows, ident[:])
@@ -122,6 +122,16 @@ def tile_easycontrolnetwork_t_kernel(tc, target_q, target_k, target_v, cond_k, c
             for k in range(2):
                 nc.tensor.matmul(s_ps[:, 1 + 2 * k, :], lhsT=bmat[:], rhs=ident32[:], is_transpose=True, start=False, stop=(k == 1))
             st[("s", n, jq)] = s_ps
+
+        def pe_warm_up():
+            warm_ps = ps_s.tile([P, 4, P], F32, tag="s")
+            for r in range(4):
+                nc.tensor.matmul(warm_ps[:, r, :], lhsT=ident32[:], rhs=ident32[:], start=True, stop=True)
+
+        def spread_bias():
+            b_ps = ps_s.tile([P, 4, P], F32, tag="s")
+            nc.tensor.matmul(b_ps[:, 0, :], lhsT=b_col[:, 0:1].to_broadcast([P, P]), rhs=ones[:], start=True, stop=True)
+            nc.vector.tensor_scalar(out=bmat[:], in0=b_ps[:, 0, :], scalar1=1.0 / SCALE, scalar2=None, op0=ALU.mult)
 
         def dve_max(n, jq):
             if jq == 0:
@@ -230,7 +240,10 @@ def tile_easycontrolnetwork_t_kernel(tc, target_q, target_k, target_v, cond_k, c
         for c, nb in enumerate(CHUNKS):
             last_head[2 * (starts[c] + nb) - 1] = c
 
-        for i in range(-2, NHEADS):
+        pe_warm_up()
+        pe_qk_transposes(0)
+        spread_bias()
+        for i in range(-1, NHEADS):
             if ok(i + 1) and (i + 1) % 4 == 2:
                 dve_qk_copy(i + 1)
             if ok(i - 2):

@@ -49,24 +49,33 @@ def tile_easycontrolnetwork_t_kernel(tc, target_q, target_k, target_v, cond_k, c
 
         loaded = {}
 
-        def load(c):
+        def load_qk(c):
             b0, nb = starts[c], CHUNKS[c]
             q = ld.tile([P, nb, 512], BF16, tag="q")
             kt = ld.tile([P, nb, 512], BF16, tag="kt")
             kc = ld.tile([P, nb, 512], BF16, tag="kc")
-            v = ld.tile([P, nb, 1024], BF16, tag="v")
             nc.sync.dma_start(out=q[:], in_=target_q[b0:b0 + nb].rearrange("b (r j) h d -> r b (j h d)", j=2))
             nc.sync.dma_start(out=kt[:], in_=target_k[b0:b0 + nb].rearrange("b (r k) h d -> r b (k h d)", k=2))
             nc.sync.dma_start(out=kc[:], in_=cond_k[b0:b0 + nb].rearrange("b (r k) h d -> r b (k h d)", k=2))
+            loaded[c] = [q, kt, kc]
+
+        def load_v(c):
+            b0, nb = starts[c], CHUNKS[c]
+            v = ld.tile([P, nb, 1024], BF16, tag="v")
             nc.sync.dma_start(out=v[0:64], in_=target_v[b0:b0 + nb].rearrange("b (r o) h d -> r b (o h d)", o=4))
             nc.sync.dma_start(out=v[64:128], in_=cond_v[b0:b0 + nb].rearrange("b (r o) h d -> r b (o h d)", o=4))
-            loaded[c] = (q, kt, kc, v)
+            loaded[c].append(v)
 
         b_col = const.tile([P, 1], BF16)
         nc.vector.memset(b_col[:], 0.0)
         nc.scalar.dma_start(out=b_col[0:1, :], in_=b_param.partition_broadcast(1))
-        for c in range(LD_BUFS):
-            load(c)
+        load_qk(0)
+        load_qk(1)
+        load_v(0)
+        load_v(1)
+        for c in range(2, LD_BUFS):
+            load_qk(c)
+            load_v(c)
 
         zero = const.tile([P, 1], F32)
         nc.vector.memset(zero[:], 0.0)
@@ -88,11 +97,11 @@ def tile_easycontrolnetwork_t_kernel(tc, target_q, target_k, target_v, cond_k, c
         def ok(n):
             return 0 <= n < NHEADS
 
-        def pe_qk_transposes(n):
+        def pe_qk_transposes(n, pool, tag):
             b, h = divmod(n, 2)
             c, bi = where[b]
-            q, kt, kc, v = loaded[c]
-            qkt_ps = ps_q.tile([P, 6, P], BF16, tag="qkt_ps")
+            q, kt, kc = loaded[c][0:3]
+            qkt_ps = pool.tile([P, 6, P], BF16, tag=tag)
             parts = [(q, 0), (q, 1), (kt, 0), (kc, 0), (kt, 1), (kc, 1)]
             for s in range(6):
                 src, j = parts[s]
@@ -241,17 +250,21 @@ def tile_easycontrolnetwork_t_kernel(tc, target_q, target_k, target_v, cond_k, c
             last_head[2 * (starts[c] + nb) - 1] = c
 
         pe_warm_up()
-        pe_qk_transposes(0)
+        pe_qk_transposes(0, ps_q, "qkt_ps")
         spread_bias()
-        for i in range(-1, NHEADS):
-            if ok(i + 1) and (i + 1) % 4 == 2:
+        pe_qk_transposes(1, ps_1, "o_ps")
+        act_qk_copy(0)
+        dve_qk_copy(1)
+        pool_regroup_v(0)
+        for i in range(NHEADS):
+            if i > 1 and ok(i + 1) and (i + 1) % 4 == 2:
                 dve_qk_copy(i + 1)
             if ok(i - 2):
                 act_exp(i - 2, 0)
                 act_exp(i - 2, 1)
             if ok(i - 3):
                 copy_et(i - 3, BOTH)
-            if ok(i + 1) and not ((i + 1) % 4 == 2):
+            if i > 0 and ok(i + 1) and not (i > 1 and (i + 1) % 4 == 2):
                 act_qk_copy(i + 1)
             if ok(i):
                 pe_scores(i, 0)
@@ -263,7 +276,7 @@ def tile_easycontrolnetwork_t_kernel(tc, target_q, target_k, target_v, cond_k, c
             if ok(i - 2):
                 pe_e_transposes(i - 2, BOTH, ps_2, "et")
             if ok(i + 2):
-                pe_qk_transposes(i + 2)
+                pe_qk_transposes(i + 2, ps_q, "qkt_ps")
             if (i - 8) % 2 == 0 and 0 <= (i - 8) // 2 < B:
                 norm((i - 8) // 2, BOTH)
             if ok(i):
@@ -279,7 +292,8 @@ def tile_easycontrolnetwork_t_kernel(tc, target_q, target_k, target_v, cond_k, c
             if ok(i + 1):
                 pool_regroup_v(i + 1)
             if (i + 1) in last_head and last_head[i + 1] + LD_BUFS < len(CHUNKS):
-                load(last_head[i + 1] + LD_BUFS)
+                load_qk(last_head[i + 1] + LD_BUFS)
+                load_v(last_head[i + 1] + LD_BUFS)
 
         n = NHEADS - 1
         b = B - 1

from contextlib import ExitStack

import concourse.mybir as mybir
from concourse.masks import make_identity

BF16 = mybir.dt.bfloat16
F32 = mybir.dt.float32
U32 = mybir.dt.uint32
U8 = mybir.dt.uint8
FP8X4 = mybir.dt.float8_e4m3fn_x4
ALU = mybir.AluOpType
ACTF = mybir.ActivationFunctionType
AX = mybir.AxisListType

B, S, H, D = 32, 256, 2, 128
P = 128
NHEADS = B * H
SCALE = D ** -0.5
FLOPS = 2 * 2 * B * H * S * (2 * S) * D

CHUNKS = [1, 1] + [2] * 15
LD_BUFS = 4
PIN = True
BOTH = (0, 1)


def tile_easycontrolnetwork_t_kernel(tc, target_q, target_k, target_v, cond_k, cond_v, b_param, out):
    nc = tc.nc
    assert sum(CHUNKS) == B
    starts = [sum(CHUNKS[:c]) for c in range(len(CHUNKS))]
    where = {}
    for c, nb in enumerate(CHUNKS):
        for bi in range(nb):
            where[starts[c] + bi] = (c, bi)

    with ExitStack() as ctx:
        const = ctx.enter_context(tc.tile_pool(name="const", bufs=1))
        ld = ctx.enter_context(tc.tile_pool(name="ld", bufs=LD_BUFS))
        work = ctx.enter_context(tc.tile_pool(name="work", bufs=3))
        outp = ctx.enter_context(tc.tile_pool(name="outp", bufs=6))
        small = ctx.enter_context(tc.tile_pool(name="small", bufs=4))
        vgp = ctx.enter_context(tc.tile_pool(name="vgp", bufs=2))
        vqp = ctx.enter_context(tc.tile_pool(name="vqp", bufs=10))
        eqp = ctx.enter_context(tc.tile_pool(name="eqp", bufs=4))
        ps_s = ctx.enter_context(tc.psum_pool(name="ps_s", bufs=4))
        ps_q = ctx.enter_context(tc.psum_pool(name="ps_q", bufs=1))
        ps_1 = ctx.enter_context(tc.psum_pool(name="ps_1", bufs=1))
        ps_2 = ctx.enter_context(tc.psum_pool(name="ps_2", bufs=2))

        loaded = {}

        def load_qk(c):
            b0, nb = starts[c], CHUNKS[c]
            q = ld.tile([P, nb, 512], BF16, tag="q")
            kt = ld.tile([P, nb, 512], BF16, tag="kt")
            kc = ld.tile([P, nb, 512], BF16, tag="kc")
            nc.sync.dma_start(out=q[:], in_=target_q[b0:b0 + nb].rearrange("b (r j) h d -> r b (j h d)", j=2))
            nc.sync.dma_start(out=kt[:], in_=target_k[b0:b0 + nb].rearrange("b (r k) h d -> r b (k h d)", k=2))
            nc.sync.dma_start(out=kc[:], in_=cond_k[b0:b0 + nb].rearrange("b (r k) h d -> r b (k h d)", k=2))
            loaded[c] = [q, kt, kc]

        def load_v(c):
            b0, nb = starts[c], CHUNKS[c]
            v = ld.tile([P, nb, 1024], BF16, tag="v")
            nc.sync.dma_start(out=v[0:64], in_=target_v[b0:b0 + nb].rearrange("b (r o) h d -> r b (o h d)", o=4))
            nc.sync.dma_start(out=v[64:128], in_=cond_v[b0:b0 + nb].rearrange("b (r o) h d -> r b (o h d)", o=4))
            loaded[c].append(v)

        b_col = const.tile([P, 1], BF16)
        nc.vector.memset(b_col[:], 0.0)
        nc.scalar.dma_start(out=b_col[0:1, :], in_=b_param.partition_broadcast(1))
        load_qk(0)
        load_qk(1)
        load_v(0)
        load_v(1)
        for c in range(2, LD_BUFS):
            load_qk(c)
            load_v(c)

        zero = const.tile([P, 1], F32)
        nc.vector.memset(zero[:], 0.0)
        exp_zero = const.tile([P, 1], F32)
        nc.scalar.activation(out=exp_zero[:], in_=zero[:], func=ACTF.Exp)
        ident32 = const.tile([P, P], F32)
        make_identity(nc, ident32[:])
        ident = const.tile([P, P], BF16)
        make_identity(nc, ident[:])
        ones = const.tile([P, P], BF16)
        nc.vector.memset(ones[:], 1.0)
        bmat = const.tile([P, P], F32)

        if PIN:
            ctx.enter_context(tc.manual_schedule())

        st = {}

        def ok(n):
            return 0 <= n < NHEADS

        def pe_qk_transposes(n, pool, tag):
            b, h = divmod(n, 2)
            c, bi = where[b]
            q, kt, kc = loaded[c][0:3]
            qkt_ps = pool.tile([P, 6, P], BF16, tag=tag)
            parts = [(q, 0), (q, 1), (kt, 0), (kc, 0), (kt, 1), (kc, 1)]
            for s in range(6):
                src, j = parts[s]
                rows = src[:, bi, j * 256 + h * 128:j * 256 + h * 128 + 128]
                if s < (6 if n < 2 else (n + 1) % 2):
                    nc.tensor.matmul(qkt_ps[:, s, :], lhsT=rows, rhs=ident[:], start=True, stop=True)
                else:
                    nc.tensor.transpose(qkt_ps[:, s, :], rows, ident[:])
            st[("qkt_ps", n)] = qkt_ps

        def dve_qk_copy(n):
            qkt = work.tile([P, 6, P], BF16, tag="qkt")
            nc.vector.tensor_copy(out=qkt[:], in_=st[("qkt_ps", n)][:])
            st[("qkt", n)] = qkt

        def act_qk_copy(n):
            qkt = work.tile([P, 6, P], BF16, tag="qkt")
            nc.scalar.copy(out=qkt[:].rearrange("p a c -> p (a c)").bitcast(F32),
                           in_=st[("qkt_ps", n)][:].rearrange("p a c -> p (a c)").bitcast(F32))
            st[("qkt", n)] = qkt

        def pe_scores(n, jq):
            qkt = st[("qkt", n)]
            s_ps = ps_s.tile([P, 4, P], F32, tag="s")
            nc.tensor.matmul(s_ps[:].rearrange("q t c -> q (t c)"), lhsT=qkt[:, jq, :],
                             rhs=qkt[:, 2:6, :].rearrange("d a c -> d (a c)"), start=True, stop=False)
            for k in range(2):
                nc.tensor.matmul(s_ps[:, 1 + 2 * k, :], lhsT=bmat[:], rhs=ident32[:], is_transpose=True, start=False, stop=(k == 1))
            st[("s", n, jq)] = s_ps

        def pe_warm_up():
            warm_ps = ps_s.tile([P, 4, P], F32, tag="s")
            for r in range(4):
                nc.tensor.matmul(warm_ps[:, r, :], lhsT=ident32[:], rhs=ident32[:], start=True, stop=True)

        def spread_bias():
            b_ps = ps_s.tile([P, 4, P], F32, tag="s")
            nc.tensor.matmul(b_ps[:, 0, :], lhsT=b_col[:, 0:1].to_broadcast([P, P]), rhs=ones[:], start=True, stop=True)
            nc.vector.tensor_scalar(out=bmat[:], in0=b_ps[:, 0, :], scalar1=1.0 / SCALE, scalar2=None, op0=ALU.mult)

        def dve_max(n, jq):
            if jq == 0:
                mx = small.tile([P, 2], F32, tag="mx")
                st[("mx", n)] = mx
            nc.vector.tensor_reduce(
                out=st[("mx", n)][:, jq:jq + 1],
                in_=st[("s", n, jq)][:].rearrange("q t c -> q (t c)"),
                axis=AX.X,
                op=ALU.max,
            )

        def dve_bias(n):
            negm = small.tile([P, 2], F32, tag="negm")
            nc.vector.tensor_scalar(out=negm[:], in0=st[("mx", n)][:], scalar1=-SCALE, scalar2=None, op0=ALU.mult)
            st[("negm", n)] = negm

        def act_exp(n, jq):
            b, h = divmod(n, 2)
            if jq == 0:
                e_new = work.tile([P, 2, 4, P], BF16, tag="e")
                st[("e", n)] = e_new
                if h == 0:
                    rs_new = small.tile([P, 2, 2], F32, tag="rs")
                    st[("rs", b)] = rs_new
            nc.scalar.activation(out=st[("e", n)][:, jq].rearrange("q t c -> q (t c)"),
                                 in_=st[("s", n, jq)][:].rearrange("q t c -> q (t c)"), func=ACTF.Exp,
                                 bias=st[("negm", n)][:, jq:jq + 1], scale=SCALE, accum_out=st[("rs", b)][:, h, jq:jq + 1])

        def pe_e_transposes(n, jqs, pool, tag):
            e = st[("e", n)]
            et_ps = pool.tile([P, 2, 2, P], F32, tag=tag)
            for jq in jqs:
                for u in range(2):
                    nc.tensor.transpose(et_ps[:, jq, u, :],
                                        e[:, jq, 2 * u:2 * u + 2, :].rearrange("q t c -> q (t c)").bitcast(F32), ident32[:])
                st[("et", n, jq)] = et_ps

        def copy_et(n, jqs):
            m = len(jqs)
            eg = work.tile([P, m, P, 4], BF16, tag="eg", align_bytes=64)
            for jq in jqs:
                st[("eg", n, jq)] = eg
            words = eg[:].rearrange("p a q t -> p (a q t)").bitcast(F32).rearrange("p (a q u) -> p a q u", a=m, u=2)
            pairs = st[("et", n, jqs[0])][:, jqs[0]:jqs[0] + m].rearrange("p a u q -> p a q u")
            nc.scalar.copy(out=words, in_=pairs)

        def dve_quant_e(n, jqs):
            m = len(jqs)
            ec = eqp.tile([P, m * P], U32, tag="ec", align_bytes=64)
            es = eqp.tile([P, m * P], U8, tag="es", align_bytes=64)
            nc.vector.quantize_mx(out=ec[:].bitcast(FP8X4), scales=es[:],
                                  in_=st[("eg", n, jqs[0])][:].rearrange("p a q t -> p (a q t)"))
            for a in range(m):
                st[("ec", n, jqs[a])] = (ec[:, P * a:P * a + P], es[:, P * a:P * a + P])

        def pool_regroup_v(n):
            b, h = divmod(n, 2)
            c, bi = where[b]
            v = loaded[c][3]
            vg = vgp.tile([P, P, 4], BF16, tag="vg", align_bytes=64)
            src = v[:, bi, :].rearrange("p (w u h d) -> p w u h d", w=2, u=2, h=2)[:, :, :, h, :]
            nc.gpsimd.tensor_scalar(out=vg[:].rearrange("p d (u w) -> p d u w", u=2), in0=src.rearrange("p w u d -> p d u w"), scalar1=1.0, scalar2=0.0,
                                    op0=ALU.mult, op1=ALU.add)
            st[("vg", n)] = vg

        def dve_quant_v(n):
            vc = vqp.tile([P, P], U32, tag="vc", align_bytes=64)
            vs = vqp.tile([P, P], U8, tag="vs", align_bytes=64)
            nc.vector.quantize_mx(out=vc[:].bitcast(FP8X4), scales=vs[:],
                                  in_=st[("vg", n)][:].rearrange("p c t -> p (c t)"))
            st[("vc", n)] = (vc, vs)

        def pe_pv(b, jqs, o_ps):
            for h in range(2):
                vc, vs = st[("vc", 2 * b + h)]
                for jq in jqs:
                    ec, es = st[("ec", 2 * b + h, jq)]
                    nc.tensor.matmul_mx(
                        out=o_ps[:, jq, h, :],
                        lhsT=ec.bitcast(FP8X4),
                        lhsT_scale=es,
                        rhs=vc[:].bitcast(FP8X4),
                        rhs_scale=vs[:],
                        start=True,
                        stop=True,
                    )
            st[("o", b)] = o_ps

        def dve_rinv(b):
            rinv = small.tile([P, 2, 2], F32, tag="rinv")
            nc.vector.reciprocal(out=rinv[:], in_=st[("rs", b)][:])
            st[("rinv", b)] = rinv

        def norm(b, jqs):
            m = len(jqs)
            j0 = jqs[0]
            osb = outp.tile([P, m, 2, P], F32, tag="osb")
            nc.vector.tensor_tensor(out=osb[:], in0=st[("o", b)][:, j0:j0 + m],
                                    in1=st[("rinv", b)][:, :, j0:j0 + m].rearrange("p h j -> p j h").unsqueeze(3).to_broadcast([P, m, 2, P]),
                                    op=ALU.mult)
            nc.sync.dma_start(out=out[b].rearrange("(r j) c -> r j c", j=2)[:, j0:j0 + m],
                              in_=osb[:].rearrange("p j h d -> p j (h d)"))

        last_head = {}
        for c, nb in enumerate(CHUNKS):
            last_head[2 * (starts[c] + nb) - 1] = c

        pe_warm_up()
        pe_qk_transposes(0, ps_q, "qkt_ps")
        spread_bias()
        pe_qk_transposes(1, ps_1, "o_ps")
        act_qk_copy(0)
        dve_qk_copy(1)
        pool_regroup_v(0)
        for i in range(NHEADS):
            if i > 1 and ok(i + 1) and (i + 1) % 4 == 2:
                dve_qk_copy(i + 1)
            if ok(i - 2):
                act_exp(i - 2, 0)
                act_exp(i - 2, 1)
            if ok(i - 3):
                copy_et(i - 3, BOTH)
            if i > 0 and ok(i + 1) and not (i > 1 and (i + 1) % 4 == 2):
                act_qk_copy(i + 1)
            if ok(i):
                pe_scores(i, 0)
            if (i - 7) % 2 == 0 and 0 <= (i - 7) // 2 < B:
                o_ps = ps_1.tile([P, 2, 2, P], F32, tag="o_ps")
                pe_pv((i - 7) // 2, BOTH, o_ps)
            if ok(i):
                pe_scores(i, 1)
            if ok(i - 2):
                pe_e_transposes(i - 2, BOTH, ps_2, "et")
            if ok(i + 2):
                pe_qk_transposes(i + 2, ps_q, "qkt_ps")
            if (i - 8) % 2 == 0 and 0 <= (i - 8) // 2 < B:
                norm((i - 8) // 2, BOTH)
            if ok(i):
                dve_max(i, 0)
                dve_max(i, 1)
            if ok(i - 4):
                dve_quant_e(i - 4, BOTH)
            if ok(i):
                dve_bias(i)
                dve_quant_v(i)
            if i % 2 == 0 and 0 <= (i - 4) // 2 < B:
                dve_rinv((i - 4) // 2)
            if ok(i + 1):
                pool_regroup_v(i + 1)
            if (i + 1) in last_head and last_head[i + 1] + LD_BUFS < len(CHUNKS):
                load_qk(last_head[i + 1] + LD_BUFS)
                load_v(last_head[i + 1] + LD_BUFS)

        n = NHEADS - 1
        b = B - 1
        act_exp(n - 1, 0)
        act_exp(n - 1, 1)
        dve_rinv(b - 1)
        copy_et(n - 2, BOTH)
        act_exp(n, 0)
        act_exp(n, 1)
        dve_quant_e(n - 3, BOTH)
        norm(b - 3, BOTH)
        pe_e_transposes(n - 1, BOTH, ps_2, "et")
        dve_quant_e(n - 2, BOTH)
        o_ps = ps_s.tile([P, 2, 2, P], F32, tag="s")
        pe_pv(b - 2, BOTH, o_ps)
        pe_e_transposes(n, (0,), ps_2, "et")
        copy_et(n - 1, BOTH)
        norm(b - 2, BOTH)
        o_ps = ps_s.tile([P, 2, 2, P], F32, tag="s")
        pe_pv(b - 1, BOTH, o_ps)
        copy_et(n, (0,))
        pe_e_transposes(n, (1,), ps_s, "s")
        copy_et(n, (1,))
        dve_quant_e(n - 1, BOTH)
        dve_rinv(b)
        dve_quant_e(n, (0,))
        dve_quant_e(n, (1,))
        norm(b - 1, BOTH)
        o_ps = ps_s.tile([P, 2, 2, P], F32, tag="s")
        pe_pv(b, (0,), o_ps)
        pe_pv(b, (1,), o_ps)
        norm(b, (0,))
        norm(b, (1,))
